import numpy as np
import ml_dtypes


def mxq(x, axis, fmt="e4m3"):
    dtype, down = {"e4m3": (ml_dtypes.float8_e4m3fn, 7), "e5m2": (ml_dtypes.float8_e5m2, 14)}[fmt]
    v = np.moveaxis(np.asarray(x, np.float32).astype(ml_dtypes.bfloat16).astype(np.float64), axis, -1)
    blocks = v.reshape(v.shape[:-1] + (-1, 32))
    amax = np.abs(blocks).max(-1, keepdims=True)
    byte = np.maximum(np.where(amax > 0, np.frexp(amax)[1] - 1 + 127, 0) - down, 1)
    scale = np.exp2(byte - 127.0)
    codes = (blocks / scale).astype(np.float32).astype(dtype).astype(np.float64)
    return np.moveaxis((codes * scale).reshape(v.shape), -1, axis)


WIDE = False


def mx_kscale(k):
    if not WIDE:
        return np.ones(k)
    levels = np.array([10, -10, 5, -5, 0])
    if k % 512:
        return np.exp2(np.random.permutation(np.resize(levels, k // 32))).repeat(32)
    a = np.empty((k // 512, 16))
    for p in range(k // 512):
        a[p, :8] = np.random.permutation(np.resize(levels, 8))
        for g in range(8):
            far = levels[np.abs(levels - a[p, g]) >= 10]
            a[p, g + 8] = far[np.random.randint(len(far))]
    return np.exp2(a.ravel()).repeat(32)


BF16 = ml_dtypes.bfloat16


def bf(x):
    return np.asarray(x, np.float32).astype(BF16)


def f64(x):
    return np.asarray(x).astype(np.float64)


N, Ci, H, W, Co = 4, 1024, 32, 32, 256
TAPS = [(1, 1), (0, 1), (1, 0), (1, 2), (2, 1)]
K = len(TAPS)
PAD = 1


def setup_inputs():
    s = mx_kscale(Ci)
    return {"x": bf(np.random.standard_normal((N, Ci, H, W)) * s[None, :, None, None]),
            "weight": bf(np.random.standard_normal((Co, Ci, K)) / np.sqrt(Ci * K) / s[None, :, None])}


def reference(x, weight):
    xq = mxq(f64(x).reshape(N, Ci, H * W), 1, "e4m3")
    wq = mxq(f64(weight), 1, "e4m3")
    outs = []
    for k, (dy, dx) in enumerate(TAPS):
        y = (wq[:, :, k] @ xq).reshape(N, Co, H, W)
        yp = np.pad(y, ((0, 0), (0, 0), (PAD, PAD), (PAD, PAD)))
        outs.append(yp[:, :, dy:dy + H, dx:dx + W])
    return np.stack(outs, axis=0).sum(axis=0)

@@ -1,0 +1,214 @@
+from contextlib import ExitStack
+
+import concourse.mybir as mybir
+from concourse.masks import make_identity
+
+BF16 = mybir.dt.bfloat16
+F32 = mybir.dt.float32
+I32 = mybir.dt.int32
+U32 = mybir.dt.uint32
+U8 = mybir.dt.uint8
+FP8X4 = mybir.dt.float8_e4m3fn_x4
+ADD = mybir.AluOpType.add
+
+IMAGES, C_IN, HEIGHT, WIDTH = 4, 1024, 32, 32
+C_OUT, TAPS = 256, 5
+P = 128
+PACK = 4
+K_PASS = P * PACK
+PASSES = C_IN // K_PASS
+O_TILES = C_OUT // P
+HALVES = 2
+HALF_ROWS = HEIGHT // HALVES
+HALF_PIX = HALF_ROWS * WIDTH
+IMAGE_PIX = HEIGHT * WIDTH
+PAD_PIX = (HEIGHT + 2) * WIDTH
+OPERANDS = PASSES * TAPS
+
+CENTRE, UP, LEFT, RIGHT, DOWN = 0, 1, 2, 3, 4
+ROW_OFFSET = {CENTRE: 0, UP: -1, LEFT: 0, RIGHT: 0, DOWN: 1}
+
+VECTOR_TAPS = 3
+VECTOR_PIX = 256
+
+FLOPS = 2 * IMAGES * HEIGHT * WIDTH * C_IN * C_OUT * TAPS
+
+
+def tile_spatialconv_pa_t_kernel(tc, x, weight, out):
+    nc = tc.nc
+    with ExitStack() as ctx:
+        keep = ctx.enter_context(tc.tile_pool(name="keep", bufs=1))
+        stage = ctx.enter_context(tc.tile_pool(name="stage", bufs=4))
+        acc_pool = ctx.enter_context(tc.psum_pool(name="acc", bufs=2))
+        flip_pool = ctx.enter_context(tc.psum_pool(name="flip", bufs=2))
+
+        w_raw = {}
+        x_raw = {}
+
+        def load_weights(m):
+            for g in range(PASSES):
+                w_raw[m, g] = keep.tile([P, K_PASS * TAPS], BF16, name="w_raw_%d_%d" % (m, g))
+                nc.sync.dma_start(
+                    out=w_raw[m, g][:],
+                    in_=weight[m * P : (m + 1) * P, g * K_PASS : (g + 1) * K_PASS, :].rearrange(
+                        "o c k -> o (c k)"
+                    ),
+                )
+
+        def load_image(n):
+            for g in range(PASSES):
+                x_raw[n, g] = keep.tile([P, PACK, IMAGE_PIX], BF16, name="x_raw_%d_%d" % (n, g))
+                nc.sync.dma_start(
+                    out=x_raw[n, g][:].rearrange("p t w -> p (t w)"),
+                    in_=x[n, g * K_PASS : (g + 1) * K_PASS, :, :].rearrange(
+                        "(p t) h w -> p (t h w)", t=PACK
+                    ),
+                )
+
+        load_weights(0)
+        load_image(0)
+        load_weights(1)
+        for n in range(1, IMAGES):
+            load_image(n)
+
+        ident = keep.tile([P, P], F32, name="ident")
+        make_identity(nc, ident[:])
+
+        x_codes = {}
+        x_scales = {}
+        x_scales_pad = {}
+        for n in range(IMAGES):
+            x_codes[n] = keep.tile([P, PASSES, PAD_PIX], U32, name="x_codes_%d" % n, align_bytes=64)
+            x_scales[n] = keep.tile([P, PASSES, IMAGE_PIX], U8, name="x_scales_%d" % n, align_bytes=64)
+            x_scales_pad[n] = keep.tile(
+                [P, PASSES, PAD_PIX], U8, name="x_scales_pad_%d" % n, align_bytes=64
+            )
+            nc.vector.memset(x_scales[n][:].bitcast(I32), 0)
+            for pad_row in (slice(0, WIDTH), slice(PAD_PIX - WIDTH, PAD_PIX)):
+                nc.vector.memset(x_codes[n][:, :, pad_row].bitcast(I32), 0)
+                nc.vector.memset(x_scales_pad[n][:, :, pad_row].bitcast(I32), 0)
+
+        w_codes = {}
+        w_scales = {}
+
+        def prepare_weights(m):
+            sorted_w = keep.tile([P, OPERANDS, K_PASS], BF16, name="sorted_w_%d" % m)
+            for g in range(PASSES):
+                by_channel = w_raw[m, g][:].rearrange("o (p u e k) -> o u p e k", u=2, e=2, k=TAPS)
+                by_tap = sorted_w[:, g * TAPS : (g + 1) * TAPS, :].rearrange(
+                    "o k (u p e) -> o u p e k", u=2, e=2
+                )
+                for u in range(2):
+                    nc.vector.tensor_copy(
+                        out=by_tap[:, u, :, :, 0:VECTOR_TAPS], in_=by_channel[:, u, :, :, 0:VECTOR_TAPS]
+                    )
+                    nc.scalar.copy(
+                        out=by_tap[:, u, :, :, VECTOR_TAPS:TAPS], in_=by_channel[:, u, :, :, VECTOR_TAPS:TAPS]
+                    )
+            sorted_words = sorted_w[:].bitcast(F32).rearrange("o a (u p) -> o a u p", u=2)
+            grouped_w = keep.tile([P, OPERANDS, PACK * P], BF16, name="grouped_w_%d" % m, align_bytes=64)
+            grouped_words = grouped_w[:].bitcast(F32)
+            w_codes[m] = keep.tile([P, OPERANDS, P], U32, name="w_codes_%d" % m, align_bytes=64)
+            w_scales[m] = keep.tile([P, OPERANDS, P], U8, name="w_scales_%d" % m, align_bytes=64)
+            for first in range(0, OPERANDS, 2):
+                pair = slice(first, first + 2)
+                flipped = flip_pool.tile([P, 2, 2, P], F32, name="flipped")
+                for a in range(2):
+                    for u in range(2):
+                        nc.tensor.transpose(
+                            out=flipped[:, a, u, :], in_=sorted_words[:, first + a, u, :], identity=ident[:]
+                        )
+                nc.scalar.copy(
+                    out=grouped_words[:, pair, :].rearrange("p a (o u) -> p a o u", u=2),
+                    in_=flipped[:].rearrange("p a u o -> p a o u"),
+                )
+                nc.vector.quantize_mx(
+                    out=w_codes[m][:, pair, :].rearrange("p a o -> p (a o)").bitcast(FP8X4),
+                    scales=w_scales[m][:, pair, :].rearrange("p a o -> p (a o)"),
+                    in_=grouped_w[:, pair, :].rearrange("p a f -> p (a f)"),
+                )
+
+        def prepare_piece(n, half, g):
+            first = half * HALF_PIX
+            grouped = stage.tile([P, HALF_PIX, PACK], BF16, name="grouped", align_bytes=64)
+            for start, stop, engine_copy in (
+                (0, VECTOR_PIX, nc.vector.tensor_copy),
+                (VECTOR_PIX, HALF_PIX, nc.scalar.copy),
+            ):
+                engine_copy(
+                    out=grouped[:, start:stop, :].rearrange("p (c i) t -> p c t i", i=4),
+                    in_=x_raw[n, g][:, :, first + start : first + stop].rearrange(
+                        "p t (c i) -> p c t i", i=4
+                    ),
+                )
+            nc.vector.quantize_mx(
+                out=x_codes[n][:, g, WIDTH + first : WIDTH + first + HALF_PIX].bitcast(FP8X4),
+                scales=x_scales[n][:, g, first : first + HALF_PIX],
+                in_=grouped[:].rearrange("p w t -> p (w t)"),
+            )
+            if g == PASSES - 1:
+                nc.vector.tensor_copy(
+                    out=x_scales_pad[n][:, :, WIDTH + first : WIDTH + first + HALF_PIX].bitcast(I32),
+                    in_=x_scales[n][:, :, first : first + HALF_PIX].bitcast(I32),
+                )
+
+        def tap_passes(acc, n, m, half, taps):
+            last = len(taps) * PASSES - 1
+            count = 0
+            for tap in taps:
+                first_row = half * HALF_ROWS + ROW_OFFSET[tap]
+                first = (first_row + 1) * WIDTH
+                for g in range(PASSES):
+                    if first_row % 2 == 0:
+                        plane = x_scales[n][:, g, first - WIDTH : first - WIDTH + HALF_PIX]
+                    else:
+                        plane = x_scales_pad[n][:, g, first : first + HALF_PIX]
+                    nc.tensor.matmul_mx(
+                        out=acc[:].rearrange("o h w -> o (h w)"),
+                        lhsT=w_codes[m][:, g * TAPS + tap, :].bitcast(FP8X4),
+                        lhsT_scale=w_scales[m][:, g * TAPS + tap, :],
+                        rhs=x_codes[n][:, g, first : first + HALF_PIX].bitcast(FP8X4),
+                        rhs_scale=plane,
+                        start=(count == 0),
+                        stop=(count == last),
+                    )
+                    count += 1
+
+        def convolve(n, m, half):
+            acc_mid = acc_pool.tile([P, HALF_ROWS, WIDTH], F32, name="acc_mid")
+            tap_passes(acc_mid, n, m, half, (CENTRE, UP, DOWN))
+            acc_left = acc_pool.tile([P, HALF_ROWS, WIDTH], F32, name="acc_left")
+            tap_passes(acc_left, n, m, half, (LEFT,))
+            acc_right = acc_pool.tile([P, HALF_ROWS, WIDTH], F32, name="acc_right")
+            tap_passes(acc_right, n, m, half, (RIGHT,))
+            result = stage.tile([P, HALF_ROWS, WIDTH], F32, name="result")
+            nc.scalar.copy(out=result[:], in_=acc_mid[:])
+            nc.vector.tensor_tensor(
+                out=result[:, :, 1:WIDTH],
+                in0=acc_left[:, :, 0 : WIDTH - 1],
+                in1=result[:, :, 1:WIDTH],
+                op=ADD,
+            )
+            nc.vector.tensor_tensor(
+                out=result[:, :, 0 : WIDTH - 1],
+                in0=acc_right[:, :, 1:WIDTH],
+                in1=result[:, :, 0 : WIDTH - 1],
+                op=ADD,
+            )
+            nc.sync.dma_start(
+                out=out[n, m * P : (m + 1) * P, half * HALF_ROWS : (half + 1) * HALF_ROWS, :],
+                in_=result[:],
+            )
+
+        pieces = [(half, g) for half in range(HALVES) for g in range(PASSES)]
+        rounds = [(m, half) for m in range(O_TILES) for half in range(HALVES)]
+        prepare_weights(0)
+        for half, g in pieces:
+            prepare_piece(0, half, g)
+        for n in range(IMAGES):
+            for (m, half), (next_half, next_g) in zip(rounds, pieces):
+                convolve(n, m, half)
+                if n == 0 and half == 0 and m + 1 < O_TILES:
+                    prepare_weights(m + 1)
+                if n + 1 < IMAGES:
+                    prepare_piece(n + 1, next_half, next_g)

@@ -9,7 +9,6 @@ I32 = mybir.dt.int32
 U32 = mybir.dt.uint32
 U8 = mybir.dt.uint8
 FP8X4 = mybir.dt.float8_e4m3fn_x4
-ADD = mybir.AluOpType.add
 
 IMAGES, C_IN, HEIGHT, WIDTH = 4, 1024, 32, 32
 C_OUT, TAPS = 256, 5
@@ -20,16 +19,23 @@ PASSES = C_IN // K_PASS
 O_TILES = C_OUT // P
 HALVES = 2
 HALF_ROWS = HEIGHT // HALVES
-HALF_PIX = HALF_ROWS * WIDTH
 IMAGE_PIX = HEIGHT * WIDTH
-PAD_PIX = (HEIGHT + 2) * WIDTH
 OPERANDS = PASSES * TAPS
 
+EVEN, ODD = 0, 1
+COLS = WIDTH // 2
+PLANE = HEIGHT * COLS
+HALF_PLANE = HALF_ROWS * COLS
+PAD_PLANE = PLANE + 2 * COLS
+EVEN_AT, ODD_AT, EVEN_NEXT_AT, ODD_LAST_AT = 0, PAD_PLANE, 2 * PAD_PLANE, 2 * PAD_PLANE + PLANE
+CODE_WORDS = 2 * PAD_PLANE + 2 * PLANE
+SETS = 3
+BASE, ABOVE, BELOW, EVEN_NEXT, ODD_LAST, SCALE_PLANES = 0, 2, 4, 6, 7, 8
+
 CENTRE, UP, LEFT, RIGHT, DOWN = 0, 1, 2, 3, 4
-ROW_OFFSET = {CENTRE: 0, UP: -1, LEFT: 0, RIGHT: 0, DOWN: 1}
+SLOT = {CENTRE: 0, UP: 1, DOWN: 2, RIGHT: 3, LEFT: 4}
 
 VECTOR_TAPS = 3
-VECTOR_PIX = 256
 
 FLOPS = 2 * IMAGES * HEIGHT * WIDTH * C_IN * C_OUT * TAPS
 
@@ -38,177 +44,335 @@ def tile_spatialconv_pa_t_kernel(tc, x, weight, out):
     nc = tc.nc
     with ExitStack() as ctx:
         keep = ctx.enter_context(tc.tile_pool(name="keep", bufs=1))
+        raws = ctx.enter_context(tc.tile_pool(name="raws", bufs=8))
+        sorts = ctx.enter_context(tc.tile_pool(name="sorts", bufs=3))
         stage = ctx.enter_context(tc.tile_pool(name="stage", bufs=4))
-        acc_pool = ctx.enter_context(tc.psum_pool(name="acc", bufs=2))
+        results = ctx.enter_context(tc.tile_pool(name="results", bufs=6))
+        acc_pool = ctx.enter_context(tc.psum_pool(name="acc", bufs=6))
         flip_pool = ctx.enter_context(tc.psum_pool(name="flip", bufs=2))
+        ctx.enter_context(tc.manual_schedule())
 
         w_raw = {}
         x_raw = {}
 
-        def load_weights(m):
-            for g in range(PASSES):
-                w_raw[m, g] = keep.tile([P, K_PASS * TAPS], BF16, name="w_raw_%d_%d" % (m, g))
+        def load_weights(m, g):
+            w_raw[m, g] = keep.tile([P, K_PASS * TAPS], BF16, name="w_raw_%d_%d" % (m, g))
+            nc.sync.dma_start(
+                out=w_raw[m, g][:],
+                in_=weight[m * P : (m + 1) * P, g * K_PASS : (g + 1) * K_PASS, :].rearrange("o c k -> o (c k)"),
+            )
+
+        def load_image(n, g, parts):
+            x_raw[n, g] = raws.tile([P, PACK, IMAGE_PIX], BF16, name="x_raw")
+            rows = HEIGHT // parts
+            for i in range(parts):
                 nc.sync.dma_start(
-                    out=w_raw[m, g][:],
-                    in_=weight[m * P : (m + 1) * P, g * K_PASS : (g + 1) * K_PASS, :].rearrange(
-                        "o c k -> o (c k)"
+                    out=x_raw[n, g][:, :, i * rows * WIDTH : (i + 1) * rows * WIDTH],
+                    in_=x[n, g * K_PASS : (g + 1) * K_PASS, i * rows : (i + 1) * rows, :].rearrange(
+                        "(p t) h w -> p t (h w)", t=PACK
                     ),
                 )
 
-        def load_image(n):
-            for g in range(PASSES):
-                x_raw[n, g] = keep.tile([P, PACK, IMAGE_PIX], BF16, name="x_raw_%d_%d" % (n, g))
-                nc.sync.dma_start(
-                    out=x_raw[n, g][:].rearrange("p t w -> p (t w)"),
-                    in_=x[n, g * K_PASS : (g + 1) * K_PASS, :, :].rearrange(
-                        "(p t) h w -> p (t h w)", t=PACK
-                    ),
-                )
-
-        load_weights(0)
-        load_image(0)
-        load_weights(1)
+        load_weights(0, 0)
+        load_image(0, 0, 2)
+        load_weights(0, 1)
+        load_image(0, 1, 1)
+        for g in range(PASSES):
+            load_weights(1, g)
         for n in range(1, IMAGES):
-            load_image(n)
+            for g in range(PASSES):
+                load_image(n, g, 1)
 
         ident = keep.tile([P, P], F32, name="ident")
         make_identity(nc, ident[:])
 
         x_codes = {}
         x_scales = {}
-        x_scales_pad = {}
-        for n in range(IMAGES):
-            x_codes[n] = keep.tile([P, PASSES, PAD_PIX], U32, name="x_codes_%d" % n, align_bytes=64)
-            x_scales[n] = keep.tile([P, PASSES, IMAGE_PIX], U8, name="x_scales_%d" % n, align_bytes=64)
-            x_scales_pad[n] = keep.tile(
-                [P, PASSES, PAD_PIX], U8, name="x_scales_pad_%d" % n, align_bytes=64
-            )
-            nc.vector.memset(x_scales[n][:].bitcast(I32), 0)
-            for pad_row in (slice(0, WIDTH), slice(PAD_PIX - WIDTH, PAD_PIX)):
-                nc.vector.memset(x_codes[n][:, :, pad_row].bitcast(I32), 0)
-                nc.vector.memset(x_scales_pad[n][:, :, pad_row].bitcast(I32), 0)
+        for n in range(SETS):
+            x_codes[n] = keep.tile([P, PASSES, CODE_WORDS], U32, name="x_codes_%d" % n, align_bytes=64)
+            x_scales[n] = keep.tile([P, PASSES, SCALE_PLANES, PLANE], U8, name="x_scales_%d" % n, align_bytes=64)
+            scale_words = x_scales[n][:].bitcast(I32)
+            nc.vector.memset(scale_words[:, :, BASE : BASE + 2, :], 0)
+            words = x_codes[n][:].bitcast(I32)
+            nc.vector.memset(words[:, :, 0:COLS], 0)
+            nc.vector.memset(words[:, :, PAD_PLANE - COLS : PAD_PLANE + COLS], 0)
+            nc.vector.memset(words[:, :, 2 * PAD_PLANE - COLS : 2 * PAD_PLANE], 0)
+            nc.vector.memset(words[:, :, EVEN_NEXT_AT + COLS - 1 : EVEN_NEXT_AT + PLANE : COLS], 0)
+            nc.vector.memset(words[:, :, ODD_LAST_AT : ODD_LAST_AT + PLANE : COLS], 0)
+            nc.vector.memset(scale_words[:, :, ABOVE : ABOVE + 2, 0 : COLS // 4], 0)
+            nc.vector.memset(scale_words[:, :, BELOW : BELOW + 2, PLANE // 4 - COLS // 4 :], 0)
+            nc.vector.memset(scale_words[:, :, EVEN_NEXT, PLANE // 4 - 1 :], 0)
+            nc.vector.memset(scale_words[:, :, ODD_LAST, 0:1], 0)
+        for n in range(SETS, IMAGES):
+            x_codes[n], x_scales[n] = x_codes[n - SETS], x_scales[n - SETS]
 
         w_codes = {}
         w_scales = {}
-
-        def prepare_weights(m):
-            sorted_w = keep.tile([P, OPERANDS, K_PASS], BF16, name="sorted_w_%d" % m)
-            for g in range(PASSES):
-                by_channel = w_raw[m, g][:].rearrange("o (p u e k) -> o u p e k", u=2, e=2, k=TAPS)
-                by_tap = sorted_w[:, g * TAPS : (g + 1) * TAPS, :].rearrange(
-                    "o k (u p e) -> o u p e k", u=2, e=2
-                )
-                for u in range(2):
-                    nc.vector.tensor_copy(
-                        out=by_tap[:, u, :, :, 0:VECTOR_TAPS], in_=by_channel[:, u, :, :, 0:VECTOR_TAPS]
-                    )
-                    nc.scalar.copy(
-                        out=by_tap[:, u, :, :, VECTOR_TAPS:TAPS], in_=by_channel[:, u, :, :, VECTOR_TAPS:TAPS]
-                    )
-            sorted_words = sorted_w[:].bitcast(F32).rearrange("o a (u p) -> o a u p", u=2)
-            grouped_w = keep.tile([P, OPERANDS, PACK * P], BF16, name="grouped_w_%d" % m, align_bytes=64)
-            grouped_words = grouped_w[:].bitcast(F32)
+        for m in range(O_TILES):
             w_codes[m] = keep.tile([P, OPERANDS, P], U32, name="w_codes_%d" % m, align_bytes=64)
             w_scales[m] = keep.tile([P, OPERANDS, P], U8, name="w_scales_%d" % m, align_bytes=64)
-            for first in range(0, OPERANDS, 2):
-                pair = slice(first, first + 2)
-                flipped = flip_pool.tile([P, 2, 2, P], F32, name="flipped")
-                for a in range(2):
-                    for u in range(2):
-                        nc.tensor.transpose(
-                            out=flipped[:, a, u, :], in_=sorted_words[:, first + a, u, :], identity=ident[:]
-                        )
-                nc.scalar.copy(
-                    out=grouped_words[:, pair, :].rearrange("p a (o u) -> p a o u", u=2),
-                    in_=flipped[:].rearrange("p a u o -> p a o u"),
-                )
-                nc.vector.quantize_mx(
-                    out=w_codes[m][:, pair, :].rearrange("p a o -> p (a o)").bitcast(FP8X4),
-                    scales=w_scales[m][:, pair, :].rearrange("p a o -> p (a o)"),
-                    in_=grouped_w[:, pair, :].rearrange("p a f -> p (a f)"),
-                )
+        sorted_w = {}
+        flipped = {}
+        grouped_w = {}
 
-        def prepare_piece(n, half, g):
-            first = half * HALF_PIX
-            grouped = stage.tile([P, HALF_PIX, PACK], BF16, name="grouped", align_bytes=64)
-            for start, stop, engine_copy in (
-                (0, VECTOR_PIX, nc.vector.tensor_copy),
-                (VECTOR_PIX, HALF_PIX, nc.scalar.copy),
-            ):
-                engine_copy(
-                    out=grouped[:, start:stop, :].rearrange("p (c i) t -> p c t i", i=4),
-                    in_=x_raw[n, g][:, :, first + start : first + stop].rearrange(
-                        "p t (c i) -> p c t i", i=4
-                    ),
-                )
-            nc.vector.quantize_mx(
-                out=x_codes[n][:, g, WIDTH + first : WIDTH + first + HALF_PIX].bitcast(FP8X4),
-                scales=x_scales[n][:, g, first : first + HALF_PIX],
-                in_=grouped[:].rearrange("p w t -> p (w t)"),
-            )
-            if g == PASSES - 1:
+        def sort_weights(m, g):
+            sorted_w[m, g] = sorts.tile([P, TAPS, K_PASS], BF16, name="sorted_w")
+            by_channel = w_raw[m, g][:].rearrange("o (p u e k) -> o u p e k", u=2, e=2, k=TAPS)
+            by_tap = sorted_w[m, g][:].rearrange("o k (u p e) -> o u p e k", u=2, e=2)
+            for u in range(2):
                 nc.vector.tensor_copy(
-                    out=x_scales_pad[n][:, :, WIDTH + first : WIDTH + first + HALF_PIX].bitcast(I32),
-                    in_=x_scales[n][:, :, first : first + HALF_PIX].bitcast(I32),
+                    out=by_tap[:, u, :, :, 0:VECTOR_TAPS], in_=by_channel[:, u, :, :, 0:VECTOR_TAPS]
+                )
+                nc.scalar.copy(
+                    out=by_tap[:, u, :, :, VECTOR_TAPS:TAPS], in_=by_channel[:, u, :, :, VECTOR_TAPS:TAPS]
                 )
 
-        def tap_passes(acc, n, m, half, taps):
-            last = len(taps) * PASSES - 1
-            count = 0
-            for tap in taps:
-                first_row = half * HALF_ROWS + ROW_OFFSET[tap]
-                first = (first_row + 1) * WIDTH
-                for g in range(PASSES):
-                    if first_row % 2 == 0:
-                        plane = x_scales[n][:, g, first - WIDTH : first - WIDTH + HALF_PIX]
-                    else:
-                        plane = x_scales_pad[n][:, g, first : first + HALF_PIX]
-                    nc.tensor.matmul_mx(
-                        out=acc[:].rearrange("o h w -> o (h w)"),
-                        lhsT=w_codes[m][:, g * TAPS + tap, :].bitcast(FP8X4),
-                        lhsT_scale=w_scales[m][:, g * TAPS + tap, :],
-                        rhs=x_codes[n][:, g, first : first + HALF_PIX].bitcast(FP8X4),
-                        rhs_scale=plane,
-                        start=(count == 0),
-                        stop=(count == last),
+        def flip_weights(m, g, group):
+            words = sorted_w[m, g][:].bitcast(F32).rearrange("o k (u p) -> o k u p", u=2)
+            bank = flip_pool.tile([P, 2, 2, P], F32, name="bank")
+            for a, tap in enumerate(group):
+                for u in range(2):
+                    nc.tensor.transpose(out=bank[:, a, u, :], in_=words[:, tap, u, :], identity=ident[:])
+            flipped[m, g, group] = bank
+
+        def regroup_weights(m, g, group, engine_copy):
+            grouped = stage.tile([P, 2, P * PACK], BF16, name="grouped_w", align_bytes=64)
+            engine_copy(
+                out=grouped[:].bitcast(F32)[:, 0 : len(group), :].rearrange("p a (o u) -> p a o u", u=2),
+                in_=flipped[m, g, group][:, 0 : len(group), :, :].rearrange("p a u o -> p a o u"),
+            )
+            grouped_w[m, g, group] = grouped
+
+        def quantize_weights(m, g, group):
+            first = g * TAPS + SLOT[group[0]]
+            slots = slice(first, first + len(group))
+            nc.vector.quantize_mx(
+                out=w_codes[m][:, slots, :].rearrange("p a o -> p (a o)").bitcast(FP8X4),
+                scales=w_scales[m][:, slots, :].rearrange("p a o -> p (a o)"),
+                in_=grouped_w[m, g, group][:, 0 : len(group), :].rearrange("p a f -> p (a f)"),
+            )
+
+        grouped_x = {}
+
+        def regroup_piece(n, g, parity, rows, vector_rows):
+            first, last = rows
+            grouped = stage.tile([P, PLANE, PACK], BF16, name="grouped_x", align_bytes=64)
+            for start, stop, engine_copy in (
+                (first, first + vector_rows, nc.vector.tensor_copy),
+                (first + vector_rows, last, nc.scalar.copy),
+            ):
+                if start < stop:
+                    engine_copy(
+                        out=grouped[:, (start - first) * COLS : (stop - first) * COLS, :].rearrange(
+                            "p (c i) t -> p c t i", i=4
+                        ),
+                        in_=x_raw[n, g][:, :, start * WIDTH : stop * WIDTH].rearrange(
+                            "p t (c i e) -> p e c t i", i=4, e=2
+                        )[:, parity],
                     )
-                    count += 1
+            grouped_x[n, g, parity, rows] = grouped
 
-        def convolve(n, m, half):
-            acc_mid = acc_pool.tile([P, HALF_ROWS, WIDTH], F32, name="acc_mid")
-            tap_passes(acc_mid, n, m, half, (CENTRE, UP, DOWN))
-            acc_left = acc_pool.tile([P, HALF_ROWS, WIDTH], F32, name="acc_left")
-            tap_passes(acc_left, n, m, half, (LEFT,))
-            acc_right = acc_pool.tile([P, HALF_ROWS, WIDTH], F32, name="acc_right")
-            tap_passes(acc_right, n, m, half, (RIGHT,))
-            result = stage.tile([P, HALF_ROWS, WIDTH], F32, name="result")
-            nc.scalar.copy(out=result[:], in_=acc_mid[:])
-            nc.vector.tensor_tensor(
-                out=result[:, :, 1:WIDTH],
-                in0=acc_left[:, :, 0 : WIDTH - 1],
-                in1=result[:, :, 1:WIDTH],
-                op=ADD,
+        def quantize_piece(n, g, parity, rows):
+            first, last = rows
+            at = (EVEN_AT, ODD_AT)[parity] + COLS
+            nc.vector.quantize_mx(
+                out=x_codes[n][:, g, at + first * COLS : at + last * COLS].bitcast(FP8X4),
+                scales=x_scales[n][:, g, BASE + parity, first * COLS : last * COLS],
+                in_=grouped_x[n, g, parity, rows][:, 0 : (last - first) * COLS, :].rearrange("p w t -> p (w t)"),
             )
-            nc.vector.tensor_tensor(
-                out=result[:, :, 0 : WIDTH - 1],
-                in0=acc_right[:, :, 1:WIDTH],
-                in1=result[:, :, 0 : WIDTH - 1],
-                op=ADD,
+
+        def shift_rows(n, g, parities):
+            first, last = parities[0], parities[-1] + 1
+            scale_words = x_scales[n][:].bitcast(I32)
+            row = COLS // 4
+            base = scale_words[:, g, BASE + first : BASE + last, :]
+            above = scale_words[:, g, ABOVE + first : ABOVE + last, :]
+            below = scale_words[:, g, BELOW + first : BELOW + last, :]
+            nc.vector.tensor_copy(out=above[:, :, row : HEIGHT * row], in_=base[:, :, 0 : (HEIGHT - 1) * row])
+            nc.vector.tensor_copy(out=below[:, :, 0 : (HEIGHT - 1) * row], in_=base[:, :, row : HEIGHT * row])
+
+        def plane_rows(n, g, at):
+            return x_codes[n][:, g, at : at + PLANE].bitcast(I32).rearrange("p (h j) -> p h j", j=COLS)
+
+        def shift_odd(n, g):
+            nc.vector.tensor_copy(
+                out=plane_rows(n, g, ODD_LAST_AT)[:, :, 1:COLS],
+                in_=plane_rows(n, g, ODD_AT + COLS)[:, :, 0 : COLS - 1],
             )
+            nc.vector.tensor_copy(
+                out=x_scales[n][:, g, ODD_LAST, 1:PLANE], in_=x_scales[n][:, g, BASE + ODD, 0 : PLANE - 1]
+            )
+
+        def shift_even(n, g):
+            nc.vector.tensor_copy(
+                out=plane_rows(n, g, EVEN_NEXT_AT)[:, :, 0 : COLS - 1],
+                in_=plane_rows(n, g, EVEN_AT + COLS)[:, :, 1:COLS],
+            )
+            nc.vector.tensor_copy(
+                out=x_scales[n][:, g, EVEN_NEXT, 0 : PLANE - 1], in_=x_scales[n][:, g, BASE + EVEN, 1:PLANE]
+            )
+
+        def multiply(acc, n, m, half, parity, taps, g):
+            for tap in taps:
+                own = (EVEN_AT, ODD_AT)[parity] + COLS
+                at, plane = {
+                    CENTRE: (own, BASE + parity),
+                    UP: (own - COLS, ABOVE + parity),
+                    DOWN: (own + COLS, BELOW + parity),
+                    LEFT: ((ODD_LAST_AT, ODD_LAST), (EVEN_AT + COLS, BASE + EVEN))[parity],
+                    RIGHT: ((ODD_AT + COLS, BASE + ODD), (EVEN_NEXT_AT, EVEN_NEXT))[parity],
+                }[tap]
+                first = half * HALF_PLANE
+                nc.tensor.matmul_mx(
+                    out=acc[:, parity, :],
+                    lhsT=w_codes[m][:, g * TAPS + SLOT[tap], :].bitcast(FP8X4),
+                    lhsT_scale=w_scales[m][:, g * TAPS + SLOT[tap], :],
+                    rhs=x_codes[n][:, g, at + first : at + first + HALF_PLANE].bitcast(FP8X4),
+                    rhs_scale=x_scales[n][:, g, plane, first : first + HALF_PLANE],
+                    start=(g == 0 and tap == CENTRE),
+                    stop=(g == PASSES - 1 and tap == LAST[parity]),
+                )
+
+        def open_bank():
+            bank = acc_pool.tile([P, 2, HALF_PLANE], F32, name="acc")
+            return bank
+
+        def finish(acc, n, m, half, engine_copy):
+            result = results.tile([P, HALF_PLANE, 2], F32, name="result")
+            engine_copy(out=result[:], in_=acc[:].rearrange("o e w -> o w e"))
             nc.sync.dma_start(
-                out=out[n, m * P : (m + 1) * P, half * HALF_ROWS : (half + 1) * HALF_ROWS, :],
-                in_=result[:],
+                out=out[n, m * P : (m + 1) * P, half * HALF_ROWS : (half + 1) * HALF_ROWS, :].rearrange(
+                    "o h w -> o (h w)"
+                ),
+                in_=result[:].rearrange("o w e -> o (w e)"),
             )
 
-        pieces = [(half, g) for half in range(HALVES) for g in range(PASSES)]
-        rounds = [(m, half) for m in range(O_TILES) for half in range(HALVES)]
-        prepare_weights(0)
-        for half, g in pieces:
-            prepare_piece(0, half, g)
-        for n in range(IMAGES):
-            for (m, half), (next_half, next_g) in zip(rounds, pieces):
-                convolve(n, m, half)
-                if n == 0 and half == 0 and m + 1 < O_TILES:
-                    prepare_weights(m + 1)
-                if n + 1 < IMAGES:
-                    prepare_piece(n + 1, next_half, next_g)
+        V, S = nc.vector.tensor_copy, nc.scalar.copy
+        A, B, C = (CENTRE, UP), (DOWN, RIGHT), (LEFT,)
+        COLUMN = (CENTRE, UP, DOWN)
+        ORDER = {EVEN: (CENTRE, UP, DOWN, RIGHT, LEFT), ODD: (CENTRE, UP, DOWN, LEFT, RIGHT)}
+        LAST = {EVEN: LEFT, ODD: RIGHT}
+        UPPER, LOWER, FULL = (0, HALF_ROWS), (HALF_ROWS, HEIGHT), (0, HEIGHT)
+
+        def both(banks, n, m, parity, taps, g):
+            for half in range(HALVES):
+                multiply(banks[half], n, m, half, parity, taps, g)
+
+        sort_weights(0, 0)
+        flip_weights(0, 0, A)
+        flip_weights(0, 0, B)
+        regroup_piece(0, 0, EVEN, UPPER, 8)
+        regroup_weights(0, 0, A, V)
+        quantize_piece(0, 0, EVEN, UPPER)
+        quantize_weights(0, 0, A)
+        regroup_weights(0, 0, B, S)
+        flip_weights(0, 0, C)
+        regroup_piece(0, 0, EVEN, LOWER, 8)
+        quantize_weights(0, 0, B)
+        regroup_weights(0, 0, C, S)
+        quantize_piece(0, 0, EVEN, LOWER)
+        shift_rows(0, 0, (EVEN,))
+        quantize_weights(0, 0, C)
+        banks = [open_bank() for half in range(HALVES)]
+        regroup_piece(0, 0, ODD, FULL, 14)
+        sort_weights(0, 1)
+        both(banks, 0, 0, EVEN, COLUMN, 0)
+        quantize_piece(0, 0, ODD, FULL)
+        flip_weights(0, 1, A)
+        flip_weights(0, 1, B)
+        regroup_piece(0, 1, EVEN, FULL, 14)
+        shift_odd(0, 0)
+        both(banks, 0, 0, EVEN, (RIGHT, LEFT), 0)
+        regroup_weights(0, 1, A, S)
+        quantize_piece(0, 1, EVEN, FULL)
+        flip_weights(0, 1, C)
+        regroup_weights(0, 1, B, S)
+        quantize_weights(0, 1, A)
+        shift_rows(0, 1, (EVEN,))
+        regroup_piece(0, 1, ODD, FULL, 14)
+        quantize_weights(0, 1, B)
+        regroup_weights(0, 1, C, S)
+        both(banks, 0, 0, EVEN, COLUMN, 1)
+        quantize_piece(0, 1, ODD, FULL)
+        sort_weights(1, 0)
+        quantize_weights(0, 1, C)
+        shift_odd(0, 1)
+        flip_weights(1, 0, A)
+        flip_weights(1, 0, B)
+        both(banks, 0, 0, EVEN, (RIGHT, LEFT), 1)
+        regroup_weights(1, 0, A, S)
+        shift_rows(0, 0, (ODD,))
+        shift_even(0, 0)
+        regroup_weights(1, 0, B, S)
+        flip_weights(1, 0, C)
+        sort_weights(1, 1)
+        both(banks, 0, 0, ODD, ORDER[ODD], 0)
+        shift_rows(0, 1, (ODD,))
+        shift_even(0, 1)
+        quantize_weights(1, 0, A)
+        quantize_weights(1, 0, B)
+        regroup_weights(1, 0, C, S)
+        flip_weights(1, 1, A)
+        flip_weights(1, 1, B)
+        both(banks, 0, 0, ODD, ORDER[ODD], 1)
+        regroup_weights(1, 1, A, S)
+        quantize_weights(1, 0, C)
+        regroup_weights(1, 1, B, S)
+        regroup_piece(1, 0, EVEN, FULL, 12)
+        quantize_weights(1, 1, A)
+        flip_weights(1, 1, C)
+        quantize_weights(1, 1, B)
+        later = [(banks[half], 0, 0, half) for half in range(HALVES)]
+        banks = [open_bank() for half in range(HALVES)]
+        both(banks, 0, 1, EVEN, ORDER[EVEN], 0)
+        regroup_weights(1, 1, C, S)
+        quantize_piece(1, 0, EVEN, FULL)
+        quantize_weights(1, 1, C)
+        regroup_piece(1, 0, ODD, FULL, 12)
+        both(banks, 0, 1, EVEN, ORDER[EVEN], 1)
+        finish(*later.pop(0), S)
+        regroup_piece(1, 1, EVEN, FULL, 12)
+        quantize_piece(1, 0, ODD, FULL)
+        finish(*later.pop(0), S)
+        both(banks, 0, 1, ODD, ORDER[ODD], 0)
+        shift_rows(1, 0, (EVEN, ODD))
+        shift_odd(1, 0)
+        regroup_piece(1, 1, ODD, FULL, 12)
+        quantize_piece(1, 1, EVEN, FULL)
+        both(banks, 0, 1, ODD, ORDER[ODD], 1)
+        quantize_piece(1, 1, ODD, FULL)
+        shift_rows(1, 1, (EVEN, ODD))
+        shift_odd(1, 1)
+        shift_even(1, 0)
+        shift_even(1, 1)
+        later += [(banks[half], 0, 1, half) for half in range(HALVES)]
+
+        for n in range(1, IMAGES):
+            quarters = [(g, parity) for g in range(PASSES) for parity in (EVEN, ODD)]
+            for m in range(O_TILES):
+                banks = [open_bank() for half in range(HALVES)]
+                for step in range(2):
+                    if m == 0:
+                        parity = (EVEN, ODD)[step]
+                        for g in range(PASSES):
+                            both(banks, n, m, parity, ORDER[parity], g)
+                    else:
+                        for parity in (EVEN, ODD):
+                            for g in range(PASSES):
+                                multiply(banks[step], n, m, step, parity, ORDER[parity], g)
+                    if n + 1 < IMAGES:
+                        g, parity = quarters.pop(0)
+                        regroup_piece(n + 1, g, parity, FULL, 10)
+                        quantize_piece(n + 1, g, parity, FULL)
+                        if parity == ODD:
+                            shift_rows(n + 1, g, (EVEN, ODD))
+                            shift_odd(n + 1, g)
+                            shift_even(n + 1, g)
+                    if later:
+                        finish(*later.pop(0), S)
+                    if m == 1:
+                        later.append((banks[step], n, m, step))
+                if m == 0:
+                    later += [(banks[half], n, m, half) for half in range(HALVES)]
+        for bank in later:
+            finish(*bank, S)

@@ -29,7 +29,7 @@ HALF_PLANE = HALF_ROWS * COLS
 PAD_PLANE = PLANE + 2 * COLS
 EVEN_AT, ODD_AT, EVEN_NEXT_AT, ODD_LAST_AT = 0, PAD_PLANE, 2 * PAD_PLANE, 2 * PAD_PLANE + PLANE
 CODE_WORDS = 2 * PAD_PLANE + 2 * PLANE
-SETS = 3
+SETS = 2
 BASE, ABOVE, BELOW, EVEN_NEXT, ODD_LAST, SCALE_PLANES = 0, 2, 4, 6, 7, 8
 
 CENTRE, UP, LEFT, RIGHT, DOWN = 0, 1, 2, 3, 4
@@ -48,8 +48,8 @@ def tile_spatialconv_pa_t_kernel(tc, x, weight, out):
         sorts = ctx.enter_context(tc.tile_pool(name="sorts", bufs=3))
         stage = ctx.enter_context(tc.tile_pool(name="stage", bufs=4))
         results = ctx.enter_context(tc.tile_pool(name="results", bufs=6))
-        acc_pool = ctx.enter_context(tc.psum_pool(name="acc", bufs=6))
-        flip_pool = ctx.enter_context(tc.psum_pool(name="flip", bufs=2))
+        acc_pool = ctx.enter_context(tc.psum_pool(name="acc", bufs=5))
+        flip_pool = ctx.enter_context(tc.psum_pool(name="flip", bufs=3))
         ctx.enter_context(tc.manual_schedule())
 
         w_raw = {}
@@ -261,12 +261,12 @@ def tile_spatialconv_pa_t_kernel(tc, x, weight, out):
         sort_weights(0, 0)
         flip_weights(0, 0, A)
         flip_weights(0, 0, B)
+        flip_weights(0, 0, C)
         regroup_piece(0, 0, EVEN, UPPER, 8)
         regroup_weights(0, 0, A, V)
         quantize_piece(0, 0, EVEN, UPPER)
         quantize_weights(0, 0, A)
         regroup_weights(0, 0, B, S)
-        flip_weights(0, 0, C)
         regroup_piece(0, 0, EVEN, LOWER, 8)
         quantize_weights(0, 0, B)
         regroup_weights(0, 0, C, S)
@@ -274,22 +274,21 @@ def tile_spatialconv_pa_t_kernel(tc, x, weight, out):
         shift_rows(0, 0, (EVEN,))
         quantize_weights(0, 0, C)
         banks = [open_bank() for half in range(HALVES)]
-        regroup_piece(0, 0, ODD, FULL, 14)
+        regroup_piece(0, 0, ODD, FULL, 16)
         sort_weights(0, 1)
         both(banks, 0, 0, EVEN, COLUMN, 0)
         quantize_piece(0, 0, ODD, FULL)
-        flip_weights(0, 1, A)
-        flip_weights(0, 1, B)
-        regroup_piece(0, 1, EVEN, FULL, 14)
+        for group in (A, B, C):
+            flip_weights(0, 1, group)
+        regroup_piece(0, 1, EVEN, FULL, 16)
         shift_odd(0, 0)
         both(banks, 0, 0, EVEN, (RIGHT, LEFT), 0)
         regroup_weights(0, 1, A, S)
         quantize_piece(0, 1, EVEN, FULL)
-        flip_weights(0, 1, C)
         regroup_weights(0, 1, B, S)
         quantize_weights(0, 1, A)
         shift_rows(0, 1, (EVEN,))
-        regroup_piece(0, 1, ODD, FULL, 14)
+        regroup_piece(0, 1, ODD, FULL, 16)
         quantize_weights(0, 1, B)
         regroup_weights(0, 1, C, S)
         both(banks, 0, 0, EVEN, COLUMN, 1)
@@ -297,14 +296,13 @@ def tile_spatialconv_pa_t_kernel(tc, x, weight, out):
         sort_weights(1, 0)
         quantize_weights(0, 1, C)
         shift_odd(0, 1)
-        flip_weights(1, 0, A)
-        flip_weights(1, 0, B)
+        for group in (A, B, C):
+            flip_weights(1, 0, group)
         both(banks, 0, 0, EVEN, (RIGHT, LEFT), 1)
         regroup_weights(1, 0, A, S)
         shift_rows(0, 0, (ODD,))
         shift_even(0, 0)
         regroup_weights(1, 0, B, S)
-        flip_weights(1, 0, C)
         sort_weights(1, 1)
         both(banks, 0, 0, ODD, ORDER[ODD], 0)
         shift_rows(0, 1, (ODD,))
@@ -312,15 +310,14 @@ def tile_spatialconv_pa_t_kernel(tc, x, weight, out):
         quantize_weights(1, 0, A)
         quantize_weights(1, 0, B)
         regroup_weights(1, 0, C, S)
-        flip_weights(1, 1, A)
-        flip_weights(1, 1, B)
+        for group in (A, B, C):
+            flip_weights(1, 1, group)
         both(banks, 0, 0, ODD, ORDER[ODD], 1)
         regroup_weights(1, 1, A, S)
         quantize_weights(1, 0, C)
         regroup_weights(1, 1, B, S)
-        regroup_piece(1, 0, EVEN, FULL, 12)
+        regroup_piece(1, 0, EVEN, FULL, 16)
         quantize_weights(1, 1, A)
-        flip_weights(1, 1, C)
         quantize_weights(1, 1, B)
         later = [(banks[half], 0, 0, half) for half in range(HALVES)]
         banks = [open_bank() for half in range(HALVES)]
@@ -328,16 +325,16 @@ def tile_spatialconv_pa_t_kernel(tc, x, weight, out):
         regroup_weights(1, 1, C, S)
         quantize_piece(1, 0, EVEN, FULL)
         quantize_weights(1, 1, C)
-        regroup_piece(1, 0, ODD, FULL, 12)
+        regroup_piece(1, 0, ODD, FULL, 16)
         both(banks, 0, 1, EVEN, ORDER[EVEN], 1)
         finish(*later.pop(0), S)
-        regroup_piece(1, 1, EVEN, FULL, 12)
+        regroup_piece(1, 1, EVEN, FULL, 16)
         quantize_piece(1, 0, ODD, FULL)
         finish(*later.pop(0), S)
         both(banks, 0, 1, ODD, ORDER[ODD], 0)
         shift_rows(1, 0, (EVEN, ODD))
         shift_odd(1, 0)
-        regroup_piece(1, 1, ODD, FULL, 12)
+        regroup_piece(1, 1, ODD, FULL, 16)
         quantize_piece(1, 1, EVEN, FULL)
         both(banks, 0, 1, ODD, ORDER[ODD], 1)
         quantize_piece(1, 1, ODD, FULL)
@@ -362,7 +359,7 @@ def tile_spatialconv_pa_t_kernel(tc, x, weight, out):
                                 multiply(banks[step], n, m, step, parity, ORDER[parity], g)
                     if n + 1 < IMAGES:
                         g, parity = quarters.pop(0)
-                        regroup_piece(n + 1, g, parity, FULL, 10)
+                        regroup_piece(n + 1, g, parity, FULL, 16)
                         quantize_piece(n + 1, g, parity, FULL)
                         if parity == ODD:
                             shift_rows(n + 1, g, (EVEN, ODD))

@@ -35,7 +35,7 @@ BASE, ABOVE, BELOW, EVEN_NEXT, ODD_LAST, SCALE_PLANES = 0, 2, 4, 6, 7, 8
 CENTRE, UP, LEFT, RIGHT, DOWN = 0, 1, 2, 3, 4
 SLOT = {CENTRE: 0, UP: 1, DOWN: 2, RIGHT: 3, LEFT: 4}
 
-VECTOR_TAPS = 3
+VECTOR_TAPS, SCALAR_TAPS = slice(0, 3), slice(3, TAPS)
 
 FLOPS = 2 * IMAGES * HEIGHT * WIDTH * C_IN * C_OUT * TAPS
 
@@ -47,7 +47,7 @@ def tile_spatialconv_pa_t_kernel(tc, x, weight, out):
         raws = ctx.enter_context(tc.tile_pool(name="raws", bufs=8))
         sorts = ctx.enter_context(tc.tile_pool(name="sorts", bufs=3))
         stage = ctx.enter_context(tc.tile_pool(name="stage", bufs=4))
-        results = ctx.enter_context(tc.tile_pool(name="results", bufs=6))
+        results = ctx.enter_context(tc.tile_pool(name="results", bufs=3))
         acc_pool = ctx.enter_context(tc.psum_pool(name="acc", bufs=5))
         flip_pool = ctx.enter_context(tc.psum_pool(name="flip", bufs=3))
         ctx.enter_context(tc.manual_schedule())
@@ -55,12 +55,16 @@ def tile_spatialconv_pa_t_kernel(tc, x, weight, out):
         w_raw = {}
         x_raw = {}
 
-        def load_weights(m, g):
+        def load_weights(m, g, parts=1):
             w_raw[m, g] = keep.tile([P, K_PASS * TAPS], BF16, name="w_raw_%d_%d" % (m, g))
-            nc.sync.dma_start(
-                out=w_raw[m, g][:],
-                in_=weight[m * P : (m + 1) * P, g * K_PASS : (g + 1) * K_PASS, :].rearrange("o c k -> o (c k)"),
-            )
+            size = K_PASS // parts
+            for i in range(parts):
+                nc.sync.dma_start(
+                    out=w_raw[m, g][:, i * size * TAPS : (i + 1) * size * TAPS],
+                    in_=weight[m * P : (m + 1) * P, g * K_PASS + i * size : g * K_PASS + (i + 1) * size, :].rearrange(
+                        "o c k -> o (c k)"
+                    ),
+                )
 
         def load_image(n, g, parts):
             x_raw[n, g] = raws.tile([P, PACK, IMAGE_PIX], BF16, name="x_raw")
@@ -73,12 +77,12 @@ def tile_spatialconv_pa_t_kernel(tc, x, weight, out):
                     ),
                 )
 
-        load_weights(0, 0)
+        load_weights(0, 0, 2)
         load_image(0, 0, 2)
+        load_weights(1, 0)
         load_weights(0, 1)
         load_image(0, 1, 1)
-        for g in range(PASSES):
-            load_weights(1, g)
+        load_weights(1, 1)
         for n in range(1, IMAGES):
             for g in range(PASSES):
                 load_image(n, g, 1)
@@ -115,17 +119,15 @@ def tile_spatialconv_pa_t_kernel(tc, x, weight, out):
         flipped = {}
         grouped_w = {}
 
-        def sort_weights(m, g):
-            sorted_w[m, g] = sorts.tile([P, TAPS, K_PASS], BF16, name="sorted_w")
+        def sort_weights(m, g, engine_copy, taps, parts=1):
+            if (m, g) not in sorted_w:
+                sorted_w[m, g] = sorts.tile([P, TAPS, K_PASS], BF16, name="sorted_w")
             by_channel = w_raw[m, g][:].rearrange("o (p u e k) -> o u p e k", u=2, e=2, k=TAPS)
             by_tap = sorted_w[m, g][:].rearrange("o k (u p e) -> o u p e k", u=2, e=2)
-            for u in range(2):
-                nc.vector.tensor_copy(
-                    out=by_tap[:, u, :, :, 0:VECTOR_TAPS], in_=by_channel[:, u, :, :, 0:VECTOR_TAPS]
-                )
-                nc.scalar.copy(
-                    out=by_tap[:, u, :, :, VECTOR_TAPS:TAPS], in_=by_channel[:, u, :, :, VECTOR_TAPS:TAPS]
-                )
+            for i in range(parts):
+                part = slice(i * P // parts, (i + 1) * P // parts)
+                for u in range(2):
+                    engine_copy(out=by_tap[:, u, part, :, taps], in_=by_channel[:, u, part, :, taps])
 
         def flip_weights(m, g, group):
             words = sorted_w[m, g][:].bitcast(F32).rearrange("o k (u p) -> o k u p", u=2)
@@ -212,9 +214,9 @@ def tile_spatialconv_pa_t_kernel(tc, x, weight, out):
                 out=x_scales[n][:, g, EVEN_NEXT, 0 : PLANE - 1], in_=x_scales[n][:, g, BASE + EVEN, 1:PLANE]
             )
 
-        def multiply(acc, n, m, half, parity, taps, g):
+        def multiply(bank, n, m, parity, taps, g, pixels=slice(0, PLANE)):
+            own = (EVEN_AT, ODD_AT)[parity] + COLS
             for tap in taps:
-                own = (EVEN_AT, ODD_AT)[parity] + COLS
                 at, plane = {
                     CENTRE: (own, BASE + parity),
                     UP: (own - COLS, ABOVE + parity),
@@ -222,154 +224,159 @@ def tile_spatialconv_pa_t_kernel(tc, x, weight, out):
                     LEFT: ((ODD_LAST_AT, ODD_LAST), (EVEN_AT + COLS, BASE + EVEN))[parity],
                     RIGHT: ((ODD_AT + COLS, BASE + ODD), (EVEN_NEXT_AT, EVEN_NEXT))[parity],
                 }[tap]
-                first = half * HALF_PLANE
                 nc.tensor.matmul_mx(
-                    out=acc[:, parity, :],
+                    out=bank[:, pixels],
                     lhsT=w_codes[m][:, g * TAPS + SLOT[tap], :].bitcast(FP8X4),
                     lhsT_scale=w_scales[m][:, g * TAPS + SLOT[tap], :],
-                    rhs=x_codes[n][:, g, at + first : at + first + HALF_PLANE].bitcast(FP8X4),
-                    rhs_scale=x_scales[n][:, g, plane, first : first + HALF_PLANE],
-                    start=(g == 0 and tap == CENTRE),
-                    stop=(g == PASSES - 1 and tap == LAST[parity]),
+                    rhs=x_codes[n][:, g, at + pixels.start : at + pixels.stop].bitcast(FP8X4),
+                    rhs_scale=x_scales[n][:, g, plane, pixels],
+                    start=(g == 0 and tap == ORDER[parity][0]),
+                    stop=(g == PASSES - 1 and tap == ORDER[parity][-1]),
                 )
 
+        planar = {}
+
         def open_bank():
-            bank = acc_pool.tile([P, 2, HALF_PLANE], F32, name="acc")
+            bank = acc_pool.tile([P, PLANE], F32, name="acc")
             return bank
 
-        def finish(acc, n, m, half, engine_copy):
-            result = results.tile([P, HALF_PLANE, 2], F32, name="result")
-            engine_copy(out=result[:], in_=acc[:].rearrange("o e w -> o w e"))
+        def empty_bank(bank, n, m, parity, pixels=slice(0, PLANE)):
+            if (n, m) not in planar:
+                planar[n, m] = results.tile([P, 2, PLANE], F32, name="planar")
+            nc.scalar.copy(out=planar[n, m][:, parity, pixels], in_=bank[:, pixels])
+
+        def store(n, m, pixels=slice(0, PLANE)):
+            result = results.tile([P, PLANE, 2], F32, name="result")
+            nc.vector.tensor_copy(
+                out=result[:, pixels, :], in_=planar[n, m][:, :, pixels].rearrange("o e w -> o w e")
+            )
+            rows = slice(pixels.start // COLS, pixels.stop // COLS)
             nc.sync.dma_start(
-                out=out[n, m * P : (m + 1) * P, half * HALF_ROWS : (half + 1) * HALF_ROWS, :].rearrange(
-                    "o h w -> o (h w)"
-                ),
-                in_=result[:].rearrange("o w e -> o (w e)"),
+                out=out[n, m * P : (m + 1) * P, rows, :].rearrange("o h w -> o (h w)"),
+                in_=result[:, pixels, :].rearrange("o w e -> o (w e)"),
             )
 
         V, S = nc.vector.tensor_copy, nc.scalar.copy
         A, B, C = (CENTRE, UP), (DOWN, RIGHT), (LEFT,)
         COLUMN = (CENTRE, UP, DOWN)
         ORDER = {EVEN: (CENTRE, UP, DOWN, RIGHT, LEFT), ODD: (CENTRE, UP, DOWN, LEFT, RIGHT)}
-        LAST = {EVEN: LEFT, ODD: RIGHT}
         UPPER, LOWER, FULL = (0, HALF_ROWS), (HALF_ROWS, HEIGHT), (0, HEIGHT)
 
-        def both(banks, n, m, parity, taps, g):
-            for half in range(HALVES):
-                multiply(banks[half], n, m, half, parity, taps, g)
-
-        sort_weights(0, 0)
-        flip_weights(0, 0, A)
-        flip_weights(0, 0, B)
-        flip_weights(0, 0, C)
-        regroup_piece(0, 0, EVEN, UPPER, 8)
-        regroup_weights(0, 0, A, V)
+        sort_weights(0, 0, V, VECTOR_TAPS, 2)
+        sort_weights(0, 0, S, SCALAR_TAPS, 2)
+        for group in (A, B, C):
+            flip_weights(0, 0, group)
+        regroup_weights(0, 0, A, S)
+        regroup_piece(0, 0, EVEN, UPPER, 16)
+        regroup_weights(0, 0, B, S)
         quantize_piece(0, 0, EVEN, UPPER)
         quantize_weights(0, 0, A)
-        regroup_weights(0, 0, B, S)
-        regroup_piece(0, 0, EVEN, LOWER, 8)
-        quantize_weights(0, 0, B)
+        regroup_piece(0, 0, EVEN, LOWER, 10)
         regroup_weights(0, 0, C, S)
+        quantize_weights(0, 0, B)
         quantize_piece(0, 0, EVEN, LOWER)
-        shift_rows(0, 0, (EVEN,))
         quantize_weights(0, 0, C)
-        banks = [open_bank() for half in range(HALVES)]
-        regroup_piece(0, 0, ODD, FULL, 16)
-        sort_weights(0, 1)
-        both(banks, 0, 0, EVEN, COLUMN, 0)
+        shift_rows(0, 0, (EVEN,))
+        banks = {(m, parity): open_bank() for m in range(O_TILES) for parity in (EVEN, ODD)}
+        multiply(banks[0, EVEN], 0, 0, EVEN, COLUMN, 0)
+        regroup_piece(0, 0, ODD, FULL, 20)
         quantize_piece(0, 0, ODD, FULL)
-        for group in (A, B, C):
-            flip_weights(0, 1, group)
-        regroup_piece(0, 1, EVEN, FULL, 16)
+        sort_weights(1, 0, S, SCALAR_TAPS)
         shift_odd(0, 0)
-        both(banks, 0, 0, EVEN, (RIGHT, LEFT), 0)
-        regroup_weights(0, 1, A, S)
-        quantize_piece(0, 1, EVEN, FULL)
-        regroup_weights(0, 1, B, S)
-        quantize_weights(0, 1, A)
-        shift_rows(0, 1, (EVEN,))
-        regroup_piece(0, 1, ODD, FULL, 16)
-        quantize_weights(0, 1, B)
-        regroup_weights(0, 1, C, S)
-        both(banks, 0, 0, EVEN, COLUMN, 1)
-        quantize_piece(0, 1, ODD, FULL)
-        sort_weights(1, 0)
-        quantize_weights(0, 1, C)
-        shift_odd(0, 1)
+        sort_weights(1, 0, V, VECTOR_TAPS)
+        multiply(banks[0, EVEN], 0, 0, EVEN, (RIGHT, LEFT), 0)
         for group in (A, B, C):
             flip_weights(1, 0, group)
-        both(banks, 0, 0, EVEN, (RIGHT, LEFT), 1)
         regroup_weights(1, 0, A, S)
         shift_rows(0, 0, (ODD,))
         shift_even(0, 0)
+        multiply(banks[0, ODD], 0, 0, ODD, ORDER[ODD], 0)
         regroup_weights(1, 0, B, S)
-        sort_weights(1, 1)
-        both(banks, 0, 0, ODD, ORDER[ODD], 0)
-        shift_rows(0, 1, (ODD,))
-        shift_even(0, 1)
         quantize_weights(1, 0, A)
+        sort_weights(0, 1, V, VECTOR_TAPS)
         quantize_weights(1, 0, B)
         regroup_weights(1, 0, C, S)
+        sort_weights(0, 1, S, SCALAR_TAPS)
+        for group in (A, B, C):
+            flip_weights(0, 1, group)
+        quantize_weights(1, 0, C)
+        multiply(banks[1, EVEN], 0, 1, EVEN, ORDER[EVEN], 0)
+        regroup_piece(0, 1, EVEN, FULL, 20)
+        regroup_weights(0, 1, A, S)
+        quantize_piece(0, 1, EVEN, FULL)
+        quantize_weights(0, 1, A)
+        regroup_weights(0, 1, B, S)
+        multiply(banks[1, ODD], 0, 1, ODD, ORDER[ODD], 0)
+        regroup_piece(0, 1, ODD, FULL, 20)
+        shift_rows(0, 1, (EVEN,))
+        quantize_weights(0, 1, B)
+        regroup_weights(0, 1, C, S)
+        quantize_piece(0, 1, ODD, FULL)
+        multiply(banks[0, EVEN], 0, 0, EVEN, COLUMN, 1)
+        quantize_weights(0, 1, C)
+        shift_odd(0, 1)
+        sort_weights(1, 1, V, VECTOR_TAPS)
+        sort_weights(1, 1, S, SCALAR_TAPS)
+        multiply(banks[0, EVEN], 0, 0, EVEN, (RIGHT, LEFT), 1)
         for group in (A, B, C):
             flip_weights(1, 1, group)
-        both(banks, 0, 0, ODD, ORDER[ODD], 1)
+        shift_rows(0, 1, (ODD,))
+        shift_even(0, 1)
         regroup_weights(1, 1, A, S)
-        quantize_weights(1, 0, C)
+        multiply(banks[0, ODD], 0, 0, ODD, ORDER[ODD], 1)
         regroup_weights(1, 1, B, S)
-        regroup_piece(1, 0, EVEN, FULL, 16)
         quantize_weights(1, 1, A)
-        quantize_weights(1, 1, B)
-        later = [(banks[half], 0, 0, half) for half in range(HALVES)]
-        banks = [open_bank() for half in range(HALVES)]
-        both(banks, 0, 1, EVEN, ORDER[EVEN], 0)
         regroup_weights(1, 1, C, S)
-        quantize_piece(1, 0, EVEN, FULL)
+        regroup_piece(1, 0, EVEN, FULL, 20)
+        quantize_weights(1, 1, B)
         quantize_weights(1, 1, C)
-        regroup_piece(1, 0, ODD, FULL, 16)
-        both(banks, 0, 1, EVEN, ORDER[EVEN], 1)
-        finish(*later.pop(0), S)
-        regroup_piece(1, 1, EVEN, FULL, 16)
+        quantize_piece(1, 0, EVEN, FULL)
+        multiply(banks[1, EVEN], 0, 1, EVEN, ORDER[EVEN], 1)
+        regroup_piece(1, 0, ODD, FULL, 20)
+        shift_rows(1, 0, (EVEN,))
+        empty_bank(banks[0, EVEN], 0, 0, EVEN)
         quantize_piece(1, 0, ODD, FULL)
-        finish(*later.pop(0), S)
-        both(banks, 0, 1, ODD, ORDER[ODD], 0)
-        shift_rows(1, 0, (EVEN, ODD))
+        empty_bank(banks[0, ODD], 0, 0, ODD)
+        multiply(banks[1, ODD], 0, 1, ODD, ORDER[ODD], 1)
         shift_odd(1, 0)
-        regroup_piece(1, 1, ODD, FULL, 16)
+        shift_rows(1, 0, (ODD,))
+        shift_even(1, 0)
+        store(0, 0)
+        regroup_piece(1, 1, EVEN, FULL, 18)
+        empty_bank(banks[1, EVEN], 0, 1, EVEN)
         quantize_piece(1, 1, EVEN, FULL)
-        both(banks, 0, 1, ODD, ORDER[ODD], 1)
+        regroup_piece(1, 1, ODD, FULL, 18)
         quantize_piece(1, 1, ODD, FULL)
         shift_rows(1, 1, (EVEN, ODD))
         shift_odd(1, 1)
-        shift_even(1, 0)
         shift_even(1, 1)
-        later += [(banks[half], 0, 1, half) for half in range(HALVES)]
+        later = [(banks[1, ODD], 0, 1, ODD)]
 
         for n in range(1, IMAGES):
+            last = n == IMAGES - 1
             quarters = [(g, parity) for g in range(PASSES) for parity in (EVEN, ODD)]
-            for m in range(O_TILES):
-                banks = [open_bank() for half in range(HALVES)]
-                for step in range(2):
-                    if m == 0:
-                        parity = (EVEN, ODD)[step]
-                        for g in range(PASSES):
-                            both(banks, n, m, parity, ORDER[parity], g)
-                    else:
-                        for parity in (EVEN, ODD):
-                            for g in range(PASSES):
-                                multiply(banks[step], n, m, step, parity, ORDER[parity], g)
-                    if n + 1 < IMAGES:
-                        g, parity = quarters.pop(0)
-                        regroup_piece(n + 1, g, parity, FULL, 16)
-                        quantize_piece(n + 1, g, parity, FULL)
-                        if parity == ODD:
-                            shift_rows(n + 1, g, (EVEN, ODD))
-                            shift_odd(n + 1, g)
-                            shift_even(n + 1, g)
-                    if later:
-                        finish(*later.pop(0), S)
-                    if m == 1:
-                        later.append((banks[step], n, m, step))
-                if m == 0:
-                    later += [(banks[half], n, m, half) for half in range(HALVES)]
-        for bank in later:
-            finish(*bank, S)
+            banks = {(m, parity): open_bank() for m in range(O_TILES) for parity in (EVEN, ODD)}
+            for g in range(PASSES):
+                for m in range(O_TILES):
+                    for parity in (EVEN, ODD):
+                        if not (last and m == O_TILES - 1 and parity == ODD):
+                            multiply(banks[m, parity], n, m, parity, ORDER[parity], g)
+                        for bank_done in later:
+                            empty_bank(*bank_done)
+                            if bank_done[-1] == ODD:
+                                store(*bank_done[1:3])
+                        later = [(banks[m, parity], n, m, parity)] if g == PASSES - 1 else []
+                    if not last:
+                        next_g, next_parity = quarters.pop(0)
+                        regroup_piece(n + 1, next_g, next_parity, FULL, 16)
+                        quantize_piece(n + 1, next_g, next_parity, FULL)
+                        if next_parity == ODD:
+                            shift_rows(n + 1, next_g, (EVEN, ODD))
+                            shift_odd(n + 1, next_g)
+                            shift_even(n + 1, next_g)
+        for half in range(HALVES):
+            pixels = slice(half * HALF_PLANE, (half + 1) * HALF_PLANE)
+            for g in range(PASSES):
+                multiply(later[0][0], n, m, ODD, ORDER[ODD], g, pixels)
+            empty_bank(*later[0], pixels)
+            store(n, m, pixels)

@@ -35,7 +35,7 @@ BASE, ABOVE, BELOW, EVEN_NEXT, ODD_LAST, SCALE_PLANES = 0, 2, 4, 6, 7, 8
 CENTRE, UP, LEFT, RIGHT, DOWN = 0, 1, 2, 3, 4
 SLOT = {CENTRE: 0, UP: 1, DOWN: 2, RIGHT: 3, LEFT: 4}
 
-VECTOR_TAPS, SCALAR_TAPS = slice(0, 3), slice(3, TAPS)
+VECTOR_TAPS, SCALAR_TAPS, ALL_TAPS = slice(0, 3), slice(3, TAPS), slice(0, TAPS)
 
 FLOPS = 2 * IMAGES * HEIGHT * WIDTH * C_IN * C_OUT * TAPS
 
@@ -259,7 +259,7 @@ def tile_spatialconv_pa_t_kernel(tc, x, weight, out):
         V, S = nc.vector.tensor_copy, nc.scalar.copy
         A, B, C = (CENTRE, UP), (DOWN, RIGHT), (LEFT,)
         COLUMN = (CENTRE, UP, DOWN)
-        ORDER = {EVEN: (CENTRE, UP, DOWN, RIGHT, LEFT), ODD: (CENTRE, UP, DOWN, LEFT, RIGHT)}
+        ORDER = {EVEN: (CENTRE, UP, DOWN, RIGHT, LEFT), ODD: (CENTRE, LEFT, RIGHT, UP, DOWN)}
         UPPER, LOWER, FULL = (0, HALF_ROWS), (HALF_ROWS, HEIGHT), (0, HEIGHT)
 
         sort_weights(0, 0, V, VECTOR_TAPS, 2)
@@ -269,87 +269,88 @@ def tile_spatialconv_pa_t_kernel(tc, x, weight, out):
         regroup_weights(0, 0, A, S)
         regroup_piece(0, 0, EVEN, UPPER, 16)
         regroup_weights(0, 0, B, S)
+        regroup_piece(0, 0, EVEN, LOWER, 10)
         quantize_piece(0, 0, EVEN, UPPER)
         quantize_weights(0, 0, A)
-        regroup_piece(0, 0, EVEN, LOWER, 10)
+        regroup_piece(0, 0, ODD, FULL, 20)
         regroup_weights(0, 0, C, S)
-        quantize_weights(0, 0, B)
         quantize_piece(0, 0, EVEN, LOWER)
-        quantize_weights(0, 0, C)
+        quantize_weights(0, 0, B)
         shift_rows(0, 0, (EVEN,))
+        quantize_piece(0, 0, ODD, FULL)
+        quantize_weights(0, 0, C)
         banks = {(m, parity): open_bank() for m in range(O_TILES) for parity in (EVEN, ODD)}
         multiply(banks[0, EVEN], 0, 0, EVEN, COLUMN, 0)
-        regroup_piece(0, 0, ODD, FULL, 20)
-        quantize_piece(0, 0, ODD, FULL)
-        sort_weights(1, 0, S, SCALAR_TAPS)
+        sort_weights(1, 0, S, ALL_TAPS)
+        shift_even(0, 0)
+        shift_rows(0, 0, (ODD,))
+        multiply(banks[0, EVEN], 0, 0, EVEN, (RIGHT,), 0)
+        multiply(banks[0, ODD], 0, 0, ODD, (CENTRE, LEFT), 0)
         shift_odd(0, 0)
-        sort_weights(1, 0, V, VECTOR_TAPS)
-        multiply(banks[0, EVEN], 0, 0, EVEN, (RIGHT, LEFT), 0)
+        sort_weights(0, 1, V, VECTOR_TAPS)
+        sort_weights(0, 1, S, SCALAR_TAPS)
+        multiply(banks[0, ODD], 0, 0, ODD, (RIGHT, UP, DOWN), 0)
         for group in (A, B, C):
             flip_weights(1, 0, group)
+        multiply(banks[0, EVEN], 0, 0, EVEN, (LEFT,), 0)
+        regroup_piece(0, 1, EVEN, FULL, 24)
         regroup_weights(1, 0, A, S)
-        shift_rows(0, 0, (ODD,))
-        shift_even(0, 0)
-        multiply(banks[0, ODD], 0, 0, ODD, ORDER[ODD], 0)
         regroup_weights(1, 0, B, S)
         quantize_weights(1, 0, A)
-        sort_weights(0, 1, V, VECTOR_TAPS)
-        quantize_weights(1, 0, B)
         regroup_weights(1, 0, C, S)
-        sort_weights(0, 1, S, SCALAR_TAPS)
+        regroup_piece(0, 1, ODD, FULL, 20)
+        quantize_weights(1, 0, B)
+        quantize_piece(0, 1, EVEN, FULL)
+        quantize_weights(1, 0, C)
         for group in (A, B, C):
             flip_weights(0, 1, group)
-        quantize_weights(1, 0, C)
         multiply(banks[1, EVEN], 0, 1, EVEN, ORDER[EVEN], 0)
-        regroup_piece(0, 1, EVEN, FULL, 20)
         regroup_weights(0, 1, A, S)
-        quantize_piece(0, 1, EVEN, FULL)
-        quantize_weights(0, 1, A)
+        quantize_piece(0, 1, ODD, FULL)
         regroup_weights(0, 1, B, S)
-        multiply(banks[1, ODD], 0, 1, ODD, ORDER[ODD], 0)
-        regroup_piece(0, 1, ODD, FULL, 20)
         shift_rows(0, 1, (EVEN,))
+        quantize_weights(0, 1, A)
+        multiply(banks[1, ODD], 0, 1, ODD, ORDER[ODD], 0)
+        sort_weights(1, 1, S, ALL_TAPS)
+        shift_even(0, 1)
         quantize_weights(0, 1, B)
         regroup_weights(0, 1, C, S)
-        quantize_piece(0, 1, ODD, FULL)
-        multiply(banks[0, EVEN], 0, 0, EVEN, COLUMN, 1)
+        shift_rows(0, 1, (ODD,))
+        regroup_piece(1, 0, EVEN, FULL, 24)
         quantize_weights(0, 1, C)
         shift_odd(0, 1)
-        sort_weights(1, 1, V, VECTOR_TAPS)
-        sort_weights(1, 1, S, SCALAR_TAPS)
-        multiply(banks[0, EVEN], 0, 0, EVEN, (RIGHT, LEFT), 1)
         for group in (A, B, C):
             flip_weights(1, 1, group)
-        shift_rows(0, 1, (ODD,))
-        shift_even(0, 1)
+        multiply(banks[0, EVEN], 0, 0, EVEN, (CENTRE, UP, DOWN, RIGHT), 1)
+        multiply(banks[0, ODD], 0, 0, ODD, (CENTRE, LEFT, RIGHT, UP, DOWN), 1)
+        multiply(banks[0, EVEN], 0, 0, EVEN, (LEFT,), 1)
+        regroup_piece(1, 0, ODD, FULL, 20)
+        quantize_piece(1, 0, EVEN, FULL)
         regroup_weights(1, 1, A, S)
-        multiply(banks[0, ODD], 0, 0, ODD, ORDER[ODD], 1)
         regroup_weights(1, 1, B, S)
         quantize_weights(1, 1, A)
         regroup_weights(1, 1, C, S)
-        regroup_piece(1, 0, EVEN, FULL, 20)
-        quantize_weights(1, 1, B)
-        quantize_weights(1, 1, C)
-        quantize_piece(1, 0, EVEN, FULL)
-        multiply(banks[1, EVEN], 0, 1, EVEN, ORDER[EVEN], 1)
-        regroup_piece(1, 0, ODD, FULL, 20)
-        shift_rows(1, 0, (EVEN,))
-        empty_bank(banks[0, EVEN], 0, 0, EVEN)
         quantize_piece(1, 0, ODD, FULL)
+        quantize_weights(1, 1, B)
+        shift_rows(1, 0, (EVEN,))
+        quantize_weights(1, 1, C)
+        multiply(banks[1, EVEN], 0, 1, EVEN, ORDER[EVEN], 1)
+        shift_even(1, 0)
+        empty_bank(banks[0, EVEN], 0, 0, EVEN)
         empty_bank(banks[0, ODD], 0, 0, ODD)
         multiply(banks[1, ODD], 0, 1, ODD, ORDER[ODD], 1)
-        shift_odd(1, 0)
         shift_rows(1, 0, (ODD,))
-        shift_even(1, 0)
-        store(0, 0)
+        shift_odd(1, 0)
         regroup_piece(1, 1, EVEN, FULL, 18)
+        regroup_piece(1, 1, ODD, FULL, 18)
         empty_bank(banks[1, EVEN], 0, 1, EVEN)
         quantize_piece(1, 1, EVEN, FULL)
-        regroup_piece(1, 1, ODD, FULL, 18)
+        store(0, 0)
         quantize_piece(1, 1, ODD, FULL)
-        shift_rows(1, 1, (EVEN, ODD))
-        shift_odd(1, 1)
+        shift_rows(1, 1, (EVEN,))
         shift_even(1, 1)
+        shift_rows(1, 1, (ODD,))
+        shift_odd(1, 1)
         later = [(banks[1, ODD], 0, 1, ODD)]
 
         for n in range(1, IMAGES):
@@ -368,7 +369,7 @@ def tile_spatialconv_pa_t_kernel(tc, x, weight, out):
                         later = [(banks[m, parity], n, m, parity)] if g == PASSES - 1 else []
                     if not last:
                         next_g, next_parity = quarters.pop(0)
-                        regroup_piece(n + 1, next_g, next_parity, FULL, 16)
+                        regroup_piece(n + 1, next_g, next_parity, FULL, 10)
                         quantize_piece(n + 1, next_g, next_parity, FULL)
                         if next_parity == ODD:
                             shift_rows(n + 1, next_g, (EVEN, ODD))
@@ -376,7 +377,8 @@ def tile_spatialconv_pa_t_kernel(tc, x, weight, out):
                             shift_even(n + 1, next_g)
         for half in range(HALVES):
             pixels = slice(half * HALF_PLANE, (half + 1) * HALF_PLANE)
+            bank = later[0][0] if half == 0 else open_bank()
             for g in range(PASSES):
-                multiply(later[0][0], n, m, ODD, ORDER[ODD], g, pixels)
-            empty_bank(*later[0], pixels)
+                multiply(bank, n, m, ODD, ORDER[ODD], g, pixels)
+            empty_bank(bank, n, m, ODD, pixels)
             store(n, m, pixels)

@@ -35,7 +35,7 @@ BASE, ABOVE, BELOW, EVEN_NEXT, ODD_LAST, SCALE_PLANES = 0, 2, 4, 6, 7, 8
 CENTRE, UP, LEFT, RIGHT, DOWN = 0, 1, 2, 3, 4
 SLOT = {CENTRE: 0, UP: 1, DOWN: 2, RIGHT: 3, LEFT: 4}
 
-VECTOR_TAPS, SCALAR_TAPS, ALL_TAPS = slice(0, 3), slice(3, TAPS), slice(0, TAPS)
+FIRST_TAPS, OTHER_TAPS = slice(0, 3), slice(3, TAPS)
 
 FLOPS = 2 * IMAGES * HEIGHT * WIDTH * C_IN * C_OUT * TAPS
 
@@ -214,7 +214,7 @@ def tile_spatialconv_pa_t_kernel(tc, x, weight, out):
                 out=x_scales[n][:, g, EVEN_NEXT, 0 : PLANE - 1], in_=x_scales[n][:, g, BASE + EVEN, 1:PLANE]
             )
 
-        def multiply(bank, n, m, parity, taps, g, pixels=slice(0, PLANE)):
+        def multiply(sums, n, m, parity, taps, g, pixels=slice(0, PLANE)):
             own = (EVEN_AT, ODD_AT)[parity] + COLS
             for tap in taps:
                 at, plane = {
@@ -225,7 +225,7 @@ def tile_spatialconv_pa_t_kernel(tc, x, weight, out):
                     RIGHT: ((ODD_AT + COLS, BASE + ODD), (EVEN_NEXT_AT, EVEN_NEXT))[parity],
                 }[tap]
                 nc.tensor.matmul_mx(
-                    out=bank[:, pixels],
+                    out=sums,
                     lhsT=w_codes[m][:, g * TAPS + SLOT[tap], :].bitcast(FP8X4),
                     lhsT_scale=w_scales[m][:, g * TAPS + SLOT[tap], :],
                     rhs=x_codes[n][:, g, at + pixels.start : at + pixels.stop].bitcast(FP8X4),
@@ -262,8 +262,8 @@ def tile_spatialconv_pa_t_kernel(tc, x, weight, out):
         ORDER = {EVEN: (CENTRE, UP, DOWN, RIGHT, LEFT), ODD: (CENTRE, LEFT, RIGHT, UP, DOWN)}
         UPPER, LOWER, FULL = (0, HALF_ROWS), (HALF_ROWS, HEIGHT), (0, HEIGHT)
 
-        sort_weights(0, 0, V, VECTOR_TAPS, 2)
-        sort_weights(0, 0, S, SCALAR_TAPS, 2)
+        sort_weights(0, 0, V, FIRST_TAPS, 2)
+        sort_weights(0, 0, S, OTHER_TAPS, 2)
         for group in (A, B, C):
             flip_weights(0, 0, group)
         regroup_weights(0, 0, A, S)
@@ -272,7 +272,7 @@ def tile_spatialconv_pa_t_kernel(tc, x, weight, out):
         regroup_piece(0, 0, EVEN, LOWER, 10)
         quantize_piece(0, 0, EVEN, UPPER)
         quantize_weights(0, 0, A)
-        regroup_piece(0, 0, ODD, FULL, 20)
+        regroup_piece(0, 0, ODD, FULL, 24)
         regroup_weights(0, 0, C, S)
         quantize_piece(0, 0, EVEN, LOWER)
         quantize_weights(0, 0, B)
@@ -280,38 +280,40 @@ def tile_spatialconv_pa_t_kernel(tc, x, weight, out):
         quantize_piece(0, 0, ODD, FULL)
         quantize_weights(0, 0, C)
         banks = {(m, parity): open_bank() for m in range(O_TILES) for parity in (EVEN, ODD)}
-        multiply(banks[0, EVEN], 0, 0, EVEN, COLUMN, 0)
-        sort_weights(1, 0, S, ALL_TAPS)
+        multiply(banks[0, EVEN][:], 0, 0, EVEN, COLUMN, 0)
+        sort_weights(1, 0, S, FIRST_TAPS)
+        sort_weights(1, 0, S, OTHER_TAPS)
         shift_even(0, 0)
         shift_rows(0, 0, (ODD,))
-        multiply(banks[0, EVEN], 0, 0, EVEN, (RIGHT,), 0)
-        multiply(banks[0, ODD], 0, 0, ODD, (CENTRE, LEFT), 0)
+        multiply(banks[0, EVEN][:], 0, 0, EVEN, (RIGHT,), 0)
+        multiply(banks[0, ODD][:], 0, 0, ODD, (CENTRE, LEFT), 0)
         shift_odd(0, 0)
-        sort_weights(0, 1, V, VECTOR_TAPS)
-        sort_weights(0, 1, S, SCALAR_TAPS)
-        multiply(banks[0, ODD], 0, 0, ODD, (RIGHT, UP, DOWN), 0)
+        sort_weights(0, 1, V, FIRST_TAPS)
+        sort_weights(0, 1, S, OTHER_TAPS)
+        multiply(banks[0, ODD][:], 0, 0, ODD, (RIGHT, UP, DOWN), 0)
         for group in (A, B, C):
             flip_weights(1, 0, group)
-        multiply(banks[0, EVEN], 0, 0, EVEN, (LEFT,), 0)
-        regroup_piece(0, 1, EVEN, FULL, 24)
+        multiply(banks[0, EVEN][:], 0, 0, EVEN, (LEFT,), 0)
+        regroup_piece(0, 1, EVEN, FULL, 28)
         regroup_weights(1, 0, A, S)
         regroup_weights(1, 0, B, S)
         quantize_weights(1, 0, A)
         regroup_weights(1, 0, C, S)
-        regroup_piece(0, 1, ODD, FULL, 20)
+        regroup_piece(0, 1, ODD, FULL, 24)
         quantize_weights(1, 0, B)
         quantize_piece(0, 1, EVEN, FULL)
         quantize_weights(1, 0, C)
         for group in (A, B, C):
             flip_weights(0, 1, group)
-        multiply(banks[1, EVEN], 0, 1, EVEN, ORDER[EVEN], 0)
+        multiply(banks[1, EVEN][:], 0, 1, EVEN, ORDER[EVEN], 0)
         regroup_weights(0, 1, A, S)
         quantize_piece(0, 1, ODD, FULL)
         regroup_weights(0, 1, B, S)
         shift_rows(0, 1, (EVEN,))
         quantize_weights(0, 1, A)
-        multiply(banks[1, ODD], 0, 1, ODD, ORDER[ODD], 0)
-        sort_weights(1, 1, S, ALL_TAPS)
+        multiply(banks[1, ODD][:], 0, 1, ODD, ORDER[ODD], 0)
+        sort_weights(1, 1, S, FIRST_TAPS)
+        sort_weights(1, 1, S, OTHER_TAPS)
         shift_even(0, 1)
         quantize_weights(0, 1, B)
         regroup_weights(0, 1, C, S)
@@ -321,9 +323,9 @@ def tile_spatialconv_pa_t_kernel(tc, x, weight, out):
         shift_odd(0, 1)
         for group in (A, B, C):
             flip_weights(1, 1, group)
-        multiply(banks[0, EVEN], 0, 0, EVEN, (CENTRE, UP, DOWN, RIGHT), 1)
-        multiply(banks[0, ODD], 0, 0, ODD, (CENTRE, LEFT, RIGHT, UP, DOWN), 1)
-        multiply(banks[0, EVEN], 0, 0, EVEN, (LEFT,), 1)
+        multiply(banks[0, EVEN][:], 0, 0, EVEN, (CENTRE, UP, DOWN, RIGHT), 1)
+        multiply(banks[0, ODD][:], 0, 0, ODD, (CENTRE, LEFT, RIGHT, UP, DOWN), 1)
+        multiply(banks[0, EVEN][:], 0, 0, EVEN, (LEFT,), 1)
         regroup_piece(1, 0, ODD, FULL, 20)
         quantize_piece(1, 0, EVEN, FULL)
         regroup_weights(1, 1, A, S)
@@ -334,11 +336,11 @@ def tile_spatialconv_pa_t_kernel(tc, x, weight, out):
         quantize_weights(1, 1, B)
         shift_rows(1, 0, (EVEN,))
         quantize_weights(1, 1, C)
-        multiply(banks[1, EVEN], 0, 1, EVEN, ORDER[EVEN], 1)
+        multiply(banks[1, EVEN][:], 0, 1, EVEN, ORDER[EVEN], 1)
         shift_even(1, 0)
         empty_bank(banks[0, EVEN], 0, 0, EVEN)
         empty_bank(banks[0, ODD], 0, 0, ODD)
-        multiply(banks[1, ODD], 0, 1, ODD, ORDER[ODD], 1)
+        multiply(banks[1, ODD][:], 0, 1, ODD, ORDER[ODD], 1)
         shift_rows(1, 0, (ODD,))
         shift_odd(1, 0)
         regroup_piece(1, 1, EVEN, FULL, 18)
@@ -356,17 +358,17 @@ def tile_spatialconv_pa_t_kernel(tc, x, weight, out):
         for n in range(1, IMAGES):
             last = n == IMAGES - 1
             quarters = [(g, parity) for g in range(PASSES) for parity in (EVEN, ODD)]
-            banks = {(m, parity): open_bank() for m in range(O_TILES) for parity in (EVEN, ODD)}
+            banks = {(m, parity): open_bank() for m in range(O_TILES - last) for parity in (EVEN, ODD)}
             for g in range(PASSES):
                 for m in range(O_TILES):
                     for parity in (EVEN, ODD):
-                        if not (last and m == O_TILES - 1 and parity == ODD):
-                            multiply(banks[m, parity], n, m, parity, ORDER[parity], g)
+                        if not (last and m == O_TILES - 1):
+                            multiply(banks[m, parity][:], n, m, parity, ORDER[parity], g)
                         for bank_done in later:
                             empty_bank(*bank_done)
                             if bank_done[-1] == ODD:
                                 store(*bank_done[1:3])
-                        later = [(banks[m, parity], n, m, parity)] if g == PASSES - 1 else []
+                        later = [(banks[m, parity], n, m, parity)] if g == PASSES - 1 and not (last and m == O_TILES - 1) else []
                     if not last:
                         next_g, next_parity = quarters.pop(0)
                         regroup_piece(n + 1, next_g, next_parity, FULL, 10)
@@ -375,10 +377,16 @@ def tile_spatialconv_pa_t_kernel(tc, x, weight, out):
                             shift_rows(n + 1, next_g, (EVEN, ODD))
                             shift_odd(n + 1, next_g)
                             shift_even(n + 1, next_g)
-        for half in range(HALVES):
-            pixels = slice(half * HALF_PLANE, (half + 1) * HALF_PLANE)
-            bank = later[0][0] if half == 0 else open_bank()
-            for g in range(PASSES):
-                multiply(bank, n, m, ODD, ORDER[ODD], g, pixels)
-            empty_bank(bank, n, m, ODD, pixels)
-            store(n, m, pixels)
+        for first, stop in ((0, 16), (16, 24), (24, 32)):
+            band = slice(first * COLS, stop * COLS)
+            size = band.stop - band.start
+            bank = acc_pool.tile([P, 2, size], F32, name="acc")
+            for parity in (EVEN, ODD):
+                for g in range(PASSES):
+                    multiply(bank[:, parity, :], n, m, parity, ORDER[parity], g, band)
+            result = results.tile([P, size, 2], F32, name="result")
+            nc.scalar.copy(out=result[:], in_=bank[:].rearrange("o e w -> o w e"))
+            nc.sync.dma_start(
+                out=out[n, m * P : (m + 1) * P, first:stop, :].rearrange("o h w -> o (h w)"),
+                in_=result[:].rearrange("o w e -> o (w e)"),
+            )

@@ -44,7 +44,6 @@ def tile_spatialconv_pa_t_kernel(tc, x, weight, out):
     nc = tc.nc
     with ExitStack() as ctx:
         keep = ctx.enter_context(tc.tile_pool(name="keep", bufs=1))
-        raws = ctx.enter_context(tc.tile_pool(name="raws", bufs=8))
         sorts = ctx.enter_context(tc.tile_pool(name="sorts", bufs=3))
         stage = ctx.enter_context(tc.tile_pool(name="stage", bufs=4))
         results = ctx.enter_context(tc.tile_pool(name="results", bufs=3))
@@ -66,26 +65,27 @@ def tile_spatialconv_pa_t_kernel(tc, x, weight, out):
                     ),
                 )
 
-        def load_image(n, g, parts):
-            x_raw[n, g] = raws.tile([P, PACK, IMAGE_PIX], BF16, name="x_raw")
-            rows = HEIGHT // parts
-            for i in range(parts):
+        def load_image(n, g, rows=HEIGHT):
+            x_raw[n, g] = []
+            for first in range(0, HEIGHT, rows):
+                part = keep.tile([P, PACK, rows * WIDTH], BF16, name="x_raw_%d_%d_%d" % (n, g, first))
                 nc.sync.dma_start(
-                    out=x_raw[n, g][:, :, i * rows * WIDTH : (i + 1) * rows * WIDTH],
-                    in_=x[n, g * K_PASS : (g + 1) * K_PASS, i * rows : (i + 1) * rows, :].rearrange(
+                    out=part[:],
+                    in_=x[n, g * K_PASS : (g + 1) * K_PASS, first : first + rows, :].rearrange(
                         "(p t) h w -> p t (h w)", t=PACK
                     ),
                 )
+                x_raw[n, g].append((first, rows, part))
 
         load_weights(0, 0, 2)
-        load_image(0, 0, 2)
+        load_image(0, 0, HALF_ROWS)
         load_weights(1, 0)
         load_weights(0, 1)
-        load_image(0, 1, 1)
+        load_image(0, 1)
         load_weights(1, 1)
         for n in range(1, IMAGES):
             for g in range(PASSES):
-                load_image(n, g, 1)
+                load_image(n, g)
 
         ident = keep.tile([P, P], F32, name="ident")
         make_identity(nc, ident[:])
@@ -159,19 +159,21 @@ def tile_spatialconv_pa_t_kernel(tc, x, weight, out):
         def regroup_piece(n, g, parity, rows, vector_rows):
             first, last = rows
             grouped = stage.tile([P, PLANE, PACK], BF16, name="grouped_x", align_bytes=64)
-            for start, stop, engine_copy in (
+            for share_first, share_last, engine_copy in (
                 (first, first + vector_rows, nc.vector.tensor_copy),
                 (first + vector_rows, last, nc.scalar.copy),
             ):
-                if start < stop:
-                    engine_copy(
-                        out=grouped[:, (start - first) * COLS : (stop - first) * COLS, :].rearrange(
-                            "p (c i) t -> p c t i", i=4
-                        ),
-                        in_=x_raw[n, g][:, :, start * WIDTH : stop * WIDTH].rearrange(
-                            "p t (c i e) -> p e c t i", i=4, e=2
-                        )[:, parity],
-                    )
+                for part_first, part_rows, part in x_raw[n, g]:
+                    start, stop = max(share_first, part_first), min(share_last, part_first + part_rows)
+                    if start < stop:
+                        engine_copy(
+                            out=grouped[:, (start - first) * COLS : (stop - first) * COLS, :].rearrange(
+                                "p (c i) t -> p c t i", i=4
+                            ),
+                            in_=part[:, :, (start - part_first) * WIDTH : (stop - part_first) * WIDTH].rearrange(
+                                "p t (c i e) -> p e c t i", i=4, e=2
+                            )[:, parity],
+                        )
             grouped_x[n, g, parity, rows] = grouped
 
         def quantize_piece(n, g, parity, rows):
@@ -256,6 +258,14 @@ def tile_spatialconv_pa_t_kernel(tc, x, weight, out):
                 in_=result[:, pixels, :].rearrange("o w e -> o (w e)"),
             )
 
+        idle_operand = keep.tile([P, PLANE], BF16, name="idle_operand")
+        nc.gpsimd.memset(idle_operand[:], 0.0)
+
+        def keep_warm(count):
+            idle = acc_pool.tile([P, PLANE], F32, name="acc")
+            for i in range(count):
+                nc.tensor.matmul(out=idle[:], lhsT=idle_operand[:, 0:P], rhs=idle_operand[:], start=True, stop=True)
+
         V, S = nc.vector.tensor_copy, nc.scalar.copy
         A, B, C = (CENTRE, UP), (DOWN, RIGHT), (LEFT,)
         COLUMN = (CENTRE, UP, DOWN)
@@ -264,20 +274,24 @@ def tile_spatialconv_pa_t_kernel(tc, x, weight, out):
 
         sort_weights(0, 0, V, FIRST_TAPS, 2)
         sort_weights(0, 0, S, OTHER_TAPS, 2)
+        keep_warm(6)
         for group in (A, B, C):
             flip_weights(0, 0, group)
+        keep_warm(3)
         regroup_weights(0, 0, A, S)
         regroup_piece(0, 0, EVEN, UPPER, 16)
+        regroup_piece(0, 0, ODD, UPPER, 16)
         regroup_weights(0, 0, B, S)
-        regroup_piece(0, 0, EVEN, LOWER, 10)
         quantize_piece(0, 0, EVEN, UPPER)
+        regroup_piece(0, 0, EVEN, LOWER, 10)
         quantize_weights(0, 0, A)
-        regroup_piece(0, 0, ODD, FULL, 24)
+        regroup_piece(0, 0, ODD, LOWER, 8)
         regroup_weights(0, 0, C, S)
         quantize_piece(0, 0, EVEN, LOWER)
         quantize_weights(0, 0, B)
         shift_rows(0, 0, (EVEN,))
-        quantize_piece(0, 0, ODD, FULL)
+        quantize_piece(0, 0, ODD, UPPER)
+        quantize_piece(0, 0, ODD, LOWER)
         quantize_weights(0, 0, C)
         banks = {(m, parity): open_bank() for m in range(O_TILES) for parity in (EVEN, ODD)}
         multiply(banks[0, EVEN][:], 0, 0, EVEN, COLUMN, 0)

@@ -87,6 +87,8 @@ def tile_spatialconv_pa_t_kernel(tc, x, weight, out):
             for g in range(PASSES):
                 load_image(n, g)
 
+        idle_operand = keep.tile([P, PLANE], BF16, name="idle_operand")
+        nc.gpsimd.memset(idle_operand[:], 0.0)
         ident = keep.tile([P, P], F32, name="ident")
         make_identity(nc, ident[:])
 
@@ -258,9 +260,6 @@ def tile_spatialconv_pa_t_kernel(tc, x, weight, out):
                 in_=result[:, pixels, :].rearrange("o w e -> o (w e)"),
             )
 
-        idle_operand = keep.tile([P, PLANE], BF16, name="idle_operand")
-        nc.gpsimd.memset(idle_operand[:], 0.0)
-
         def keep_warm(count):
             idle = acc_pool.tile([P, PLANE], F32, name="acc")
             for i in range(count):
@@ -274,7 +273,7 @@ def tile_spatialconv_pa_t_kernel(tc, x, weight, out):
 
         sort_weights(0, 0, V, FIRST_TAPS, 2)
         sort_weights(0, 0, S, OTHER_TAPS, 2)
-        keep_warm(6)
+        keep_warm(4)
         for group in (A, B, C):
             flip_weights(0, 0, group)
         keep_warm(3)
@@ -285,11 +284,11 @@ def tile_spatialconv_pa_t_kernel(tc, x, weight, out):
         quantize_piece(0, 0, EVEN, UPPER)
         regroup_piece(0, 0, EVEN, LOWER, 10)
         quantize_weights(0, 0, A)
-        regroup_piece(0, 0, ODD, LOWER, 8)
         regroup_weights(0, 0, C, S)
         quantize_piece(0, 0, EVEN, LOWER)
         quantize_weights(0, 0, B)
         shift_rows(0, 0, (EVEN,))
+        regroup_piece(0, 0, ODD, LOWER, 16)
         quantize_piece(0, 0, ODD, UPPER)
         quantize_piece(0, 0, ODD, LOWER)
         quantize_weights(0, 0, C)
@@ -340,16 +339,16 @@ def tile_spatialconv_pa_t_kernel(tc, x, weight, out):
         multiply(banks[0, EVEN][:], 0, 0, EVEN, (CENTRE, UP, DOWN, RIGHT), 1)
         multiply(banks[0, ODD][:], 0, 0, ODD, (CENTRE, LEFT, RIGHT, UP, DOWN), 1)
         multiply(banks[0, EVEN][:], 0, 0, EVEN, (LEFT,), 1)
-        regroup_piece(1, 0, ODD, FULL, 20)
-        quantize_piece(1, 0, EVEN, FULL)
         regroup_weights(1, 1, A, S)
         regroup_weights(1, 1, B, S)
         quantize_weights(1, 1, A)
-        regroup_weights(1, 1, C, S)
-        quantize_piece(1, 0, ODD, FULL)
+        regroup_piece(1, 0, ODD, FULL, 20)
         quantize_weights(1, 1, B)
-        shift_rows(1, 0, (EVEN,))
+        regroup_weights(1, 1, C, S)
+        quantize_piece(1, 0, EVEN, FULL)
         quantize_weights(1, 1, C)
+        quantize_piece(1, 0, ODD, FULL)
+        shift_rows(1, 0, (EVEN,))
         multiply(banks[1, EVEN][:], 0, 1, EVEN, ORDER[EVEN], 1)
         shift_even(1, 0)
         empty_bank(banks[0, EVEN], 0, 0, EVEN)
@@ -371,26 +370,25 @@ def tile_spatialconv_pa_t_kernel(tc, x, weight, out):
 
         for n in range(1, IMAGES):
             last = n == IMAGES - 1
-            quarters = [(g, parity) for g in range(PASSES) for parity in (EVEN, ODD)]
             banks = {(m, parity): open_bank() for m in range(O_TILES - last) for parity in (EVEN, ODD)}
             for g in range(PASSES):
                 for m in range(O_TILES):
                     for parity in (EVEN, ODD):
                         if not (last and m == O_TILES - 1):
                             multiply(banks[m, parity][:], n, m, parity, ORDER[parity], g)
+                        if not last and m == 0:
+                            regroup_piece(n + 1, g, parity, FULL, 12)
+                        if not last and m == 1:
+                            quantize_piece(n + 1, g, parity, FULL)
                         for bank_done in later:
                             empty_bank(*bank_done)
                             if bank_done[-1] == ODD:
                                 store(*bank_done[1:3])
+                        if not last and m == 1 and parity == ODD:
+                            shift_even(n + 1, g)
+                            shift_rows(n + 1, g, (EVEN, ODD))
+                            shift_odd(n + 1, g)
                         later = [(banks[m, parity], n, m, parity)] if g == PASSES - 1 and not (last and m == O_TILES - 1) else []
-                    if not last:
-                        next_g, next_parity = quarters.pop(0)
-                        regroup_piece(n + 1, next_g, next_parity, FULL, 10)
-                        quantize_piece(n + 1, next_g, next_parity, FULL)
-                        if next_parity == ODD:
-                            shift_rows(n + 1, next_g, (EVEN, ODD))
-                            shift_odd(n + 1, next_g)
-                            shift_even(n + 1, next_g)
         for first, stop in ((0, 16), (16, 24), (24, 32)):
             band = slice(first * COLS, stop * COLS)
             size = band.stop - band.start

from contextlib import ExitStack

import concourse.mybir as mybir
from concourse.masks import make_identity

BF16 = mybir.dt.bfloat16
F32 = mybir.dt.float32
I32 = mybir.dt.int32
U32 = mybir.dt.uint32
U8 = mybir.dt.uint8
FP8X4 = mybir.dt.float8_e4m3fn_x4

IMAGES, C_IN, HEIGHT, WIDTH = 4, 1024, 32, 32
C_OUT, TAPS = 256, 5
P = 128
PACK = 4
K_PASS = P * PACK
PASSES = C_IN // K_PASS
O_TILES = C_OUT // P
HALVES = 2
HALF_ROWS = HEIGHT // HALVES
IMAGE_PIX = HEIGHT * WIDTH
OPERANDS = PASSES * TAPS

EVEN, ODD = 0, 1
COLS = WIDTH // 2
PLANE = HEIGHT * COLS
HALF_PLANE = HALF_ROWS * COLS
PAD_PLANE = PLANE + 2 * COLS
EVEN_AT, ODD_AT, EVEN_NEXT_AT, ODD_LAST_AT = 0, PAD_PLANE, 2 * PAD_PLANE, 2 * PAD_PLANE + PLANE
CODE_WORDS = 2 * PAD_PLANE + 2 * PLANE
SETS = 2
BASE, ABOVE, BELOW, EVEN_NEXT, ODD_LAST, SCALE_PLANES = 0, 2, 4, 6, 7, 8

CENTRE, UP, LEFT, RIGHT, DOWN = 0, 1, 2, 3, 4
SLOT = {CENTRE: 0, UP: 1, DOWN: 2, RIGHT: 3, LEFT: 4}

FIRST_TAPS, OTHER_TAPS = slice(0, 3), slice(3, TAPS)

FLOPS = 2 * IMAGES * HEIGHT * WIDTH * C_IN * C_OUT * TAPS


def tile_spatialconv_pa_t_kernel(tc, x, weight, out):
    nc = tc.nc
    with ExitStack() as ctx:
        keep = ctx.enter_context(tc.tile_pool(name="keep", bufs=1))
        sorts = ctx.enter_context(tc.tile_pool(name="sorts", bufs=3))
        stage = ctx.enter_context(tc.tile_pool(name="stage", bufs=4))
        results = ctx.enter_context(tc.tile_pool(name="results", bufs=3))
        acc_pool = ctx.enter_context(tc.psum_pool(name="acc", bufs=5))
        flip_pool = ctx.enter_context(tc.psum_pool(name="flip", bufs=3))
        ctx.enter_context(tc.manual_schedule())

        w_raw = {}
        x_raw = {}

        def load_weights(m, g, parts=1):
            w_raw[m, g] = keep.tile([P, K_PASS * TAPS], BF16, name="w_raw_%d_%d" % (m, g))
            size = K_PASS // parts
            for i in range(parts):
                nc.sync.dma_start(
                    out=w_raw[m, g][:, i * size * TAPS : (i + 1) * size * TAPS],
                    in_=weight[m * P : (m + 1) * P, g * K_PASS + i * size : g * K_PASS + (i + 1) * size, :].rearrange(
                        "o c k -> o (c k)"
                    ),
                )

        def load_image(n, g, rows=HEIGHT):
            x_raw[n, g] = []
            for first in range(0, HEIGHT, rows):
                part = keep.tile([P, PACK, rows * WIDTH], BF16, name="x_raw_%d_%d_%d" % (n, g, first))
                nc.sync.dma_start(
                    out=part[:],
                    in_=x[n, g * K_PASS : (g + 1) * K_PASS, first : first + rows, :].rearrange(
                        "(p t) h w -> p t (h w)", t=PACK
                    ),
                )
                x_raw[n, g].append((first, rows, part))

        load_weights(0, 0, 2)
        load_image(0, 0, HALF_ROWS)
        load_weights(1, 0)
        load_weights(0, 1)
        load_image(0, 1)
        load_weights(1, 1)
        for n in range(1, IMAGES):
            for g in range(PASSES):
                load_image(n, g)

        idle_operand = keep.tile([P, PLANE], BF16, name="idle_operand")
        nc.gpsimd.memset(idle_operand[:], 0.0)
        ident = keep.tile([P, P], F32, name="ident")
        make_identity(nc, ident[:])

        x_codes = {}
        x_scales = {}
        for n in range(SETS):
            x_codes[n] = keep.tile([P, PASSES, CODE_WORDS], U32, name="x_codes_%d" % n, align_bytes=64)
            x_scales[n] = keep.tile([P, PASSES, SCALE_PLANES, PLANE], U8, name="x_scales_%d" % n, align_bytes=64)
            scale_words = x_scales[n][:].bitcast(I32)
            nc.vector.memset(scale_words[:, :, BASE : BASE + 2, :], 0)
            words = x_codes[n][:].bitcast(I32)
            nc.vector.memset(words[:, :, 0:COLS], 0)
            nc.vector.memset(words[:, :, PAD_PLANE - COLS : PAD_PLANE + COLS], 0)
            nc.vector.memset(words[:, :, 2 * PAD_PLANE - COLS : 2 * PAD_PLANE], 0)
            nc.vector.memset(words[:, :, EVEN_NEXT_AT + COLS - 1 : EVEN_NEXT_AT + PLANE : COLS], 0)
            nc.vector.memset(words[:, :, ODD_LAST_AT : ODD_LAST_AT + PLANE : COLS], 0)
            nc.vector.memset(scale_words[:, :, ABOVE : ABOVE + 2, 0 : COLS // 4], 0)
            nc.vector.memset(scale_words[:, :, BELOW : BELOW + 2, PLANE // 4 - COLS // 4 :], 0)
            nc.vector.memset(scale_words[:, :, EVEN_NEXT, PLANE // 4 - 1 :], 0)
            nc.vector.memset(scale_words[:, :, ODD_LAST, 0:1], 0)
        for n in range(SETS, IMAGES):
            x_codes[n], x_scales[n] = x_codes[n - SETS], x_scales[n - SETS]

        w_codes = {}
        w_scales = {}
        for m in range(O_TILES):
            w_codes[m] = keep.tile([P, OPERANDS, P], U32, name="w_codes_%d" % m, align_bytes=64)
            w_scales[m] = keep.tile([P, OPERANDS, P], U8, name="w_scales_%d" % m, align_bytes=64)
        sorted_w = {}
        flipped = {}
        grouped_w = {}

        def sort_weights(m, g, engine_copy, taps, parts=1):
            if (m, g) not in sorted_w:
                sorted_w[m, g] = sorts.tile([P, TAPS, K_PASS], BF16, name="sorted_w")
            by_channel = w_raw[m, g][:].rearrange("o (p u e k) -> o u p e k", u=2, e=2, k=TAPS)
            by_tap = sorted_w[m, g][:].rearrange("o k (u p e) -> o u p e k", u=2, e=2)
            for i in range(parts):
                part = slice(i * P // parts, (i + 1) * P // parts)
                for u in range(2):
                    engine_copy(out=by_tap[:, u, part, :, taps], in_=by_channel[:, u, part, :, taps])

        def flip_weights(m, g, group):
            words = sorted_w[m, g][:].bitcast(F32).rearrange("o k (u p) -> o k u p", u=2)
            bank = flip_pool.tile([P, 2, 2, P], F32, name="bank")
            for a, tap in enumerate(group):
                for u in range(2):
                    nc.tensor.transpose(out=bank[:, a, u, :], in_=words[:, tap, u, :], identity=ident[:])
            flipped[m, g, group] = bank

        def regroup_weights(m, g, group, engine_copy):
            grouped = stage.tile([P, 2, P * PACK], BF16, name="grouped_w", align_bytes=64)
            engine_copy(
                out=grouped[:].bitcast(F32)[:, 0 : len(group), :].rearrange("p a (o u) -> p a o u", u=2),
                in_=flipped[m, g, group][:, 0 : len(group), :, :].rearrange("p a u o -> p a o u"),
            )
            grouped_w[m, g, group] = grouped

        def quantize_weights(m, g, group):
            first = g * TAPS + SLOT[group[0]]
            slots = slice(first, first + len(group))
            nc.vector.quantize_mx(
                out=w_codes[m][:, slots, :].rearrange("p a o -> p (a o)").bitcast(FP8X4),
                scales=w_scales[m][:, slots, :].rearrange("p a o -> p (a o)"),
                in_=grouped_w[m, g, group][:, 0 : len(group), :].rearrange("p a f -> p (a f)"),
            )

        grouped_x = {}

        def regroup_piece(n, g, parity, rows, vector_rows):
            first, last = rows
            grouped = stage.tile([P, PLANE, PACK], BF16, name="grouped_x", align_bytes=64)
            for share_first, share_last, engine_copy in (
                (first, first + vector_rows, nc.vector.tensor_copy),
                (first + vector_rows, last, nc.scalar.copy),
            ):
                for part_first, part_rows, part in x_raw[n, g]:
                    start, stop = max(share_first, part_first), min(share_last, part_first + part_rows)
                    if start < stop:
                        engine_copy(
                            out=grouped[:, (start - first) * COLS : (stop - first) * COLS, :].rearrange(
                                "p (c i) t -> p c t i", i=4
                            ),
                            in_=part[:, :, (start - part_first) * WIDTH : (stop - part_first) * WIDTH].rearrange(
                                "p t (c i e) -> p e c t i", i=4, e=2
                            )[:, parity],
                        )
            grouped_x[n, g, parity, rows] = grouped

        def quantize_piece(n, g, parity, rows):
            first, last = rows
            at = (EVEN_AT, ODD_AT)[parity] + COLS
            nc.vector.quantize_mx(
                out=x_codes[n][:, g, at + first * COLS : at + last * COLS].bitcast(FP8X4),
                scales=x_scales[n][:, g, BASE + parity, first * COLS : last * COLS],
                in_=grouped_x[n, g, parity, rows][:, 0 : (last - first) * COLS, :].rearrange("p w t -> p (w t)"),
            )

        def shift_rows(n, g, parities):
            first, last = parities[0], parities[-1] + 1
            scale_words = x_scales[n][:].bitcast(I32)
            row = COLS // 4
            base = scale_words[:, g, BASE + first : BASE + last, :]
            above = scale_words[:, g, ABOVE + first : ABOVE + last, :]
            below = scale_words[:, g, BELOW + first : BELOW + last, :]
            nc.vector.tensor_copy(out=above[:, :, row : HEIGHT * row], in_=base[:, :, 0 : (HEIGHT - 1) * row])
            nc.vector.tensor_copy(out=below[:, :, 0 : (HEIGHT - 1) * row], in_=base[:, :, row : HEIGHT * row])

        def plane_rows(n, g, at):
            return x_codes[n][:, g, at : at + PLANE].bitcast(I32).rearrange("p (h j) -> p h j", j=COLS)

        def shift_odd(n, g):
            nc.vector.tensor_copy(
                out=plane_rows(n, g, ODD_LAST_AT)[:, :, 1:COLS],
                in_=plane_rows(n, g, ODD_AT + COLS)[:, :, 0 : COLS - 1],
            )
            nc.vector.tensor_copy(
                out=x_scales[n][:, g, ODD_LAST, 1:PLANE], in_=x_scales[n][:, g, BASE + ODD, 0 : PLANE - 1]
            )

        def shift_even(n, g):
            nc.vector.tensor_copy(
                out=plane_rows(n, g, EVEN_NEXT_AT)[:, :, 0 : COLS - 1],
                in_=plane_rows(n, g, EVEN_AT + COLS)[:, :, 1:COLS],
            )
            nc.vector.tensor_copy(
                out=x_scales[n][:, g, EVEN_NEXT, 0 : PLANE - 1], in_=x_scales[n][:, g, BASE + EVEN, 1:PLANE]
            )

        def multiply(sums, n, m, parity, taps, g, pixels=slice(0, PLANE)):
            own = (EVEN_AT, ODD_AT)[parity] + COLS
            for tap in taps:
                at, plane = {
                    CENTRE: (own, BASE + parity),
                    UP: (own - COLS, ABOVE + parity),
                    DOWN: (own + COLS, BELOW + parity),
                    LEFT: ((ODD_LAST_AT, ODD_LAST), (EVEN_AT + COLS, BASE + EVEN))[parity],
                    RIGHT: ((ODD_AT + COLS, BASE + ODD), (EVEN_NEXT_AT, EVEN_NEXT))[parity],
                }[tap]
                nc.tensor.matmul_mx(
                    out=sums,
                    lhsT=w_codes[m][:, g * TAPS + SLOT[tap], :].bitcast(FP8X4),
                    lhsT_scale=w_scales[m][:, g * TAPS + SLOT[tap], :],
                    rhs=x_codes[n][:, g, at + pixels.start : at + pixels.stop].bitcast(FP8X4),
                    rhs_scale=x_scales[n][:, g, plane, pixels],
                    start=(g == 0 and tap == ORDER[parity][0]),
                    stop=(g == PASSES - 1 and tap == ORDER[parity][-1]),
                )

        planar = {}

        def open_bank():
            bank = acc_pool.tile([P, PLANE], F32, name="acc")
            return bank

        def empty_bank(bank, n, m, parity, pixels=slice(0, PLANE)):
            if (n, m) not in planar:
                planar[n, m] = results.tile([P, 2, PLANE], F32, name="planar")
            nc.scalar.copy(out=planar[n, m][:, parity, pixels], in_=bank[:, pixels])

        def store(n, m, pixels=slice(0, PLANE)):
            result = results.tile([P, PLANE, 2], F32, name="result")
            nc.vector.tensor_copy(
                out=result[:, pixels, :], in_=planar[n, m][:, :, pixels].rearrange("o e w -> o w e")
            )
            rows = slice(pixels.start // COLS, pixels.stop // COLS)
            nc.sync.dma_start(
                out=out[n, m * P : (m + 1) * P, rows, :].rearrange("o h w -> o (h w)"),
                in_=result[:, pixels, :].rearrange("o w e -> o (w e)"),
            )

        def keep_warm(count):
            idle = acc_pool.tile([P, PLANE], F32, name="acc")
            for i in range(count):
                nc.tensor.matmul(out=idle[:], lhsT=idle_operand[:, 0:P], rhs=idle_operand[:], start=True, stop=True)

        V, S = nc.vector.tensor_copy, nc.scalar.copy
        A, B, C = (CENTRE, UP), (DOWN, RIGHT), (LEFT,)
        COLUMN = (CENTRE, UP, DOWN)
        ORDER = {EVEN: (CENTRE, UP, DOWN, RIGHT, LEFT), ODD: (CENTRE, LEFT, RIGHT, UP, DOWN)}
        UPPER, LOWER, FULL = (0, HALF_ROWS), (HALF_ROWS, HEIGHT), (0, HEIGHT)

        sort_weights(0, 0, V, FIRST_TAPS, 2)
        sort_weights(0, 0, S, OTHER_TAPS, 2)
        keep_warm(4)
        for group in (A, B, C):
            flip_weights(0, 0, group)
        keep_warm(3)
        regroup_weights(0, 0, A, S)
        regroup_piece(0, 0, EVEN, UPPER, 16)
        regroup_piece(0, 0, ODD, UPPER, 16)
        regroup_weights(0, 0, B, S)
        quantize_piece(0, 0, EVEN, UPPER)
        regroup_piece(0, 0, EVEN, LOWER, 10)
        quantize_weights(0, 0, A)
        regroup_weights(0, 0, C, S)
        quantize_piece(0, 0, EVEN, LOWER)
        quantize_weights(0, 0, B)
        shift_rows(0, 0, (EVEN,))
        regroup_piece(0, 0, ODD, LOWER, 16)
        quantize_piece(0, 0, ODD, UPPER)
        quantize_piece(0, 0, ODD, LOWER)
        quantize_weights(0, 0, C)
        banks = {(m, parity): open_bank() for m in range(O_TILES) for parity in (EVEN, ODD)}
        multiply(banks[0, EVEN][:], 0, 0, EVEN, COLUMN, 0)
        sort_weights(1, 0, S, FIRST_TAPS)
        sort_weights(1, 0, S, OTHER_TAPS)
        shift_even(0, 0)
        shift_rows(0, 0, (ODD,))
        multiply(banks[0, EVEN][:], 0, 0, EVEN, (RIGHT,), 0)
        multiply(banks[0, ODD][:], 0, 0, ODD, (CENTRE, LEFT), 0)
        shift_odd(0, 0)
        sort_weights(0, 1, V, FIRST_TAPS)
        sort_weights(0, 1, S, OTHER_TAPS)
        multiply(banks[0, ODD][:], 0, 0, ODD, (RIGHT, UP, DOWN), 0)
        for group in (A, B, C):
            flip_weights(1, 0, group)
        multiply(banks[0, EVEN][:], 0, 0, EVEN, (LEFT,), 0)
        regroup_piece(0, 1, EVEN, FULL, 28)
        regroup_weights(1, 0, A, S)
        regroup_weights(1, 0, B, S)
        quantize_weights(1, 0, A)
        regroup_weights(1, 0, C, S)
        regroup_piece(0, 1, ODD, FULL, 24)
        quantize_weights(1, 0, B)
        quantize_piece(0, 1, EVEN, FULL)
        quantize_weights(1, 0, C)
        for group in (A, B, C):
            flip_weights(0, 1, group)
        multiply(banks[1, EVEN][:], 0, 1, EVEN, ORDER[EVEN], 0)
        regroup_weights(0, 1, A, S)
        quantize_piece(0, 1, ODD, FULL)
        regroup_weights(0, 1, B, S)
        shift_rows(0, 1, (EVEN,))
        quantize_weights(0, 1, A)
        multiply(banks[1, ODD][:], 0, 1, ODD, ORDER[ODD], 0)
        sort_weights(1, 1, S, FIRST_TAPS)
        sort_weights(1, 1, S, OTHER_TAPS)
        shift_even(0, 1)
        quantize_weights(0, 1, B)
        regroup_weights(0, 1, C, S)
        shift_rows(0, 1, (ODD,))
        regroup_piece(1, 0, EVEN, FULL, 24)
        quantize_weights(0, 1, C)
        shift_odd(0, 1)
        for group in (A, B, C):
            flip_weights(1, 1, group)
        multiply(banks[0, EVEN][:], 0, 0, EVEN, (CENTRE, UP, DOWN, RIGHT), 1)
        multiply(banks[0, ODD][:], 0, 0, ODD, (CENTRE, LEFT, RIGHT, UP, DOWN), 1)
        multiply(banks[0, EVEN][:], 0, 0, EVEN, (LEFT,), 1)
        regroup_weights(1, 1, A, S)
        regroup_weights(1, 1, B, S)
        quantize_weights(1, 1, A)
        regroup_piece(1, 0, ODD, FULL, 20)
        quantize_weights(1, 1, B)
        regroup_weights(1, 1, C, S)
        quantize_piece(1, 0, EVEN, FULL)
        quantize_weights(1, 1, C)
        quantize_piece(1, 0, ODD, FULL)
        shift_rows(1, 0, (EVEN,))
        multiply(banks[1, EVEN][:], 0, 1, EVEN, ORDER[EVEN], 1)
        shift_even(1, 0)
        empty_bank(banks[0, EVEN], 0, 0, EVEN)
        empty_bank(banks[0, ODD], 0, 0, ODD)
        multiply(banks[1, ODD][:], 0, 1, ODD, ORDER[ODD], 1)
        shift_rows(1, 0, (ODD,))
        shift_odd(1, 0)
        regroup_piece(1, 1, EVEN, FULL, 18)
        regroup_piece(1, 1, ODD, FULL, 18)
        empty_bank(banks[1, EVEN], 0, 1, EVEN)
        quantize_piece(1, 1, EVEN, FULL)
        store(0, 0)
        quantize_piece(1, 1, ODD, FULL)
        shift_rows(1, 1, (EVEN,))
        shift_even(1, 1)
        shift_rows(1, 1, (ODD,))
        shift_odd(1, 1)
        later = [(banks[1, ODD], 0, 1, ODD)]

        for n in range(1, IMAGES):
            last = n == IMAGES - 1
            banks = {(m, parity): open_bank() for m in range(O_TILES - last) for parity in (EVEN, ODD)}
            for g in range(PASSES):
                for m in range(O_TILES):
                    for parity in (EVEN, ODD):
                        if not (last and m == O_TILES - 1):
                            multiply(banks[m, parity][:], n, m, parity, ORDER[parity], g)
                        if not last and m == 0:
                            regroup_piece(n + 1, g, parity, FULL, 12)
                        if not last and m == 1:
                            quantize_piece(n + 1, g, parity, FULL)
                        for bank_done in later:
                            empty_bank(*bank_done)
                            if bank_done[-1] == ODD:
                                store(*bank_done[1:3])
                        if not last and m == 1 and parity == ODD:
                            shift_even(n + 1, g)
                            shift_rows(n + 1, g, (EVEN, ODD))
                            shift_odd(n + 1, g)
                        later = [(banks[m, parity], n, m, parity)] if g == PASSES - 1 and not (last and m == O_TILES - 1) else []
        for first, stop in ((0, 16), (16, 24), (24, 32)):
            band = slice(first * COLS, stop * COLS)
            size = band.stop - band.start
            bank = acc_pool.tile([P, 2, size], F32, name="acc")
            for parity in (EVEN, ODD):
                for g in range(PASSES):
                    multiply(bank[:, parity, :], n, m, parity, ORDER[parity], g, band)
            result = results.tile([P, size, 2], F32, name="result")
            nc.scalar.copy(out=result[:], in_=bank[:].rearrange("o e w -> o w e"))
            nc.sync.dma_start(
                out=out[n, m * P : (m + 1) * P, first:stop, :].rearrange("o h w -> o (h w)"),
                in_=result[:].rearrange("o w e -> o (w e)"),
            )
